import numpy as np
import ml_dtypes


def mxq(x, axis, fmt="e4m3"):
    dtype, down = {"e4m3": (ml_dtypes.float8_e4m3fn, 7), "e5m2": (ml_dtypes.float8_e5m2, 14)}[fmt]
    v = np.moveaxis(np.asarray(x, np.float32).astype(ml_dtypes.bfloat16).astype(np.float64), axis, -1)
    blocks = v.reshape(v.shape[:-1] + (-1, 32))
    amax = np.abs(blocks).max(-1, keepdims=True)
    byte = np.maximum(np.where(amax > 0, np.frexp(amax)[1] - 1 + 127, 0) - down, 1)
    scale = np.exp2(byte - 127.0)
    codes = (blocks / scale).astype(np.float32).astype(dtype).astype(np.float64)
    return np.moveaxis((codes * scale).reshape(v.shape), -1, axis)


WIDE = False


def mx_kscale(k):
    if not WIDE:
        return np.ones(k)
    levels = np.array([10, -10, 5, -5, 0])
    a = np.random.permutation(np.resize(levels, k // 512 * 4)).reshape(k // 512, 4)
    idx = np.arange(k)
    return np.exp2(a[idx // 512, idx % 128 // 32])


BF16 = ml_dtypes.bfloat16


def bf(x):
    return np.asarray(x, np.float32).astype(BF16)


def f64(x):
    return np.asarray(x).astype(np.float64)


E2M1 = np.array([0.0, 0.5, 1.0, 1.5, 2.0, 3.0, 4.0, 6.0, -0.0, -0.5, -1.0, -1.5, -2.0, -3.0, -4.0, -6.0])


def pack_weight(w, fmt):
    k, n = w.shape
    w = f64(bf(w)).reshape(k // 32, 32, n)
    amax = np.abs(w).max(1)
    if fmt == "e4m3":
        byte = np.frexp(amax)[1] - 1 + 127 - 7
    else:
        mant, ex = np.frexp(amax / 6.0)
        byte = np.where(mant > 0.5, ex, ex - 1) + 127
    byte = np.clip(np.where(amax > 0, byte, 1), 1, 254)
    scaled = (w * np.exp2(127.0 - byte)[:, None, :]).reshape(k, n).astype(np.float32)
    by_word = np.ascontiguousarray(scaled.reshape(k // 512, 128, 4, n).transpose(0, 1, 3, 2))
    if fmt == "e4m3":
        words = by_word.astype(ml_dtypes.float8_e4m3fn).view(np.uint8)
    else:
        c = by_word.astype(ml_dtypes.float4_e2m1fn).view(np.uint8) & 0xF
        words = c[..., 0::2] | (c[..., 1::2] << 4)
    return np.ascontiguousarray(words), np.ascontiguousarray(byte.astype(np.uint8).reshape(k // 512, 16, n))


def unpack_weight(words, scales, fmt):
    g, p, n, _ = words.shape
    if fmt == "e4m3":
        vals = np.ascontiguousarray(words).view(ml_dtypes.float8_e4m3fn).astype(np.float64)
    else:
        nib = np.empty((g, p, n, 4), np.uint8)
        nib[..., 0::2] = words & 0xF
        nib[..., 1::2] = words >> 4
        vals = E2M1[nib]
    vals = vals * np.repeat(np.exp2(scales.astype(np.float64) - 127.0), 8, axis=1)[..., None]
    return vals.transpose(0, 1, 3, 2).reshape(g * 512, n)

def pack4(w):
    words, scales = pack_weight(w, "e2m1")
    return words.reshape(words.shape[0], 128, -1), scales


def unpack4(words, scales):
    return unpack_weight(words.reshape(words.shape[0], 128, -1, 2), scales, "e2m1")


B, T, C, F = 8, 1024, 1024, 512
M = T


def silu(v):
    return v / (1.0 + np.exp(-v))


def sigmoid(v):
    return 1.0 / (1.0 + np.exp(-v))


def setup_inputs():
    t = mx_kscale(F)
    x = np.random.standard_normal((B, T, C)) + 0.5 * np.random.standard_normal((B, 1, C))
    h = bf(silu(np.random.standard_normal((B, T, F)) * 0.85) * t)
    memory = bf(np.random.standard_normal((1, M, C)) * 6.0 / np.sqrt(C))
    w2_words, w2_scales = pack4(np.random.standard_normal((F, C)) * 3.0 / np.sqrt(F) / t[:, None])
    b2 = bf(np.random.standard_normal(C) * 0.5)
    return {"h": h,
            "x": bf(x),
            "memory": memory,
            "w2_words": w2_words,
            "w2_scales": w2_scales,
            "b2": b2}


def reference(h, x, memory, w2_words, w2_scales, b2):
    update_gate = sigmoid((mxq(f64(h), 2, "e4m3") @ unpack4(w2_words, w2_scales)) + f64(b2))
    x_mean = f64(x).mean(axis=1, keepdims=True)
    new_mem = f64(memory) * (1.0 - update_gate) + x_mean * update_gate
    return new_mem.mean(axis=0, keepdims=True)

@@ -1,0 +1,250 @@
+from contextlib import ExitStack
+
+import concourse.mybir as mybir
+from concourse.masks import make_identity
+
+F32 = mybir.dt.float32
+BF16 = mybir.dt.bfloat16
+I32 = mybir.dt.int32
+U32 = mybir.dt.uint32
+U8 = mybir.dt.uint8
+FP8X4 = mybir.dt.float8_e4m3fn_x4
+FP4X4 = mybir.dt.float4_e2m1fn_x4
+ALU = mybir.AluOpType
+ACT = mybir.ActivationFunctionType
+
+P = 128
+B = 8
+T = 1024
+C = 1024
+K = 512
+PACK = 4
+J = T // P
+CT = C // P
+PAIRS = CT // 2
+BANK = 512
+HALVES = T // BANK
+ONES_N = 32
+TENSOR_PAIR = PAIRS - 1
+
+FLOPS = 2 * B * T * K * C
+
+
+def tile_dynamicmemorybank_pb_t_kernel(tc, h, x, memory, w2_words, w2_scales, b2, out):
+    nc = tc.nc
+    h_rows = h.rearrange("b (p j) k -> b p j k", j=J)
+    x_rows = x.rearrange("b (p j) c -> b p j c", j=J)
+    mem_rows = memory.rearrange("o (p j) c -> (o p) j c", j=J)
+    out_rows = out.rearrange("o (p j) c -> (o p) j c", j=J)
+
+    with ExitStack() as ctx:
+        const = ctx.enter_context(tc.tile_pool(name="const", bufs=1))
+        h_pool = ctx.enter_context(tc.tile_pool(name="h_pool", bufs=2))
+        x_pool = ctx.enter_context(tc.tile_pool(name="x_pool", bufs=3))
+        q_pool = ctx.enter_context(tc.tile_pool(name="q_pool", bufs=2))
+        gate_pool = ctx.enter_context(tc.tile_pool(name="gate_pool", bufs=3))
+        term_pool = ctx.enter_context(tc.tile_pool(name="term_pool", bufs=3))
+        store_pool = ctx.enter_context(tc.tile_pool(name="store_pool", bufs=3))
+        z_psum = ctx.enter_context(tc.psum_pool(name="z_psum", bufs=2))
+        work_psum = ctx.enter_context(tc.psum_pool(name="work_psum", bufs=2))
+        held_psum = ctx.enter_context(tc.psum_pool(name="held_psum", bufs=1))
+
+        ident_f32 = const.tile([P, P], F32)
+        make_identity(nc, ident_f32[:])
+        ident_bf16 = const.tile([P, P], BF16)
+        make_identity(nc, ident_bf16[:])
+        ones = const.tile([P, ONES_N], BF16)
+        nc.vector.memset(ones[:], 1.0)
+
+        warm = const.tile([P, 1], F32)
+        nc.vector.memset(warm[:], 0.0)
+        nc.scalar.activation(out=warm[:], in_=warm[:], func=ACT.Sigmoid)
+
+        w_words = const.tile([P, 2 * C], U8, align_bytes=64)
+        nc.sync.dma_start(
+            out=w_words[:].bitcast(I32),
+            in_=w2_words.rearrange("g p n -> (g p) n").bitcast(I32),
+        )
+        w_scales = const.tile([P, C], U8, align_bytes=64)
+        nc.vector.memset(w_scales[:].bitcast(I32), 0)
+        scale_rows = w2_scales.rearrange("g q n -> (g q) n")
+        for quad in range(4):
+            nc.sync.dma_start(
+                out=w_scales[32 * quad : 32 * quad + 4, :].bitcast(I32),
+                in_=scale_rows[4 * quad : 4 * quad + 4, :].bitcast(I32),
+            )
+
+        b2_rows = const.tile([P, P], BF16)
+        nc.vector.memset(b2_rows[:], 0.0)
+        nc.sync.dma_start(out=b2_rows[0:CT, :], in_=b2.rearrange("(r c) -> r c", r=CT))
+        b2_psum = work_psum.tile([P, P], BF16, tag="work")
+        nc.tensor.transpose(out=b2_psum[:], in_=b2_rows[:], identity=ident_bf16[:])
+        b2_col = const.tile([P, CT], F32)
+        nc.vector.tensor_copy(out=b2_col[:], in_=b2_psum[:, 0:CT])
+
+        def load_batch(b):
+            h_sb = h_pool.tile([P, J, K], BF16, name="h_sb")
+            nc.sync.dma_start(out=h_sb[:], in_=h_rows[b])
+            x_sb = x_pool.tile([P, J, C], BF16, name="x_sb")
+            nc.sync.dma_start(out=x_sb[:], in_=x_rows[b])
+            return h_sb, x_sb
+
+        loaded = load_batch(0)
+        mem_sb = const.tile([P, J, C], BF16)
+        nc.sync.dma_start(out=mem_sb[:], in_=mem_rows)
+
+        mem_neg = const.tile([P, CT, T], BF16)
+        for ct in range(CT):
+            memT_psum = work_psum.tile([P, T], BF16, tag="work")
+            for j in range(J):
+                nc.tensor.transpose(
+                    out=memT_psum[:, j * P : (j + 1) * P],
+                    in_=mem_sb[:, j, ct * P : (ct + 1) * P],
+                    identity=ident_bf16[:],
+                )
+            nc.scalar.mul(out=mem_neg[:, ct, :], in_=memT_psum[:], mul=-1.0 / B)
+
+        xm_neg = const.tile([P, B, CT], F32)
+
+        def prepare_batch(b, h_sb, x_sb):
+            h_pairs = h_sb[:].bitcast(F32)
+            grouped = q_pool.tile([P, J, P, PACK], BF16, name="grouped", align_bytes=64)
+            grouped_pairs = grouped[:].bitcast(F32)
+            for j0 in range(0, J, 2):
+                hT_psum = work_psum.tile([P, 2, 2, P], F32, tag="work")
+                for jj in range(2):
+                    for u in range(2):
+                        nc.tensor.transpose(
+                            out=hT_psum[:, jj, u, :],
+                            in_=h_pairs[:, j0 + jj, u : K // 2 : 2],
+                            identity=ident_f32[:],
+                        )
+                nc.scalar.copy(
+                    out=grouped_pairs[:, j0 : j0 + 2, :, :],
+                    in_=hT_psum[:].rearrange("q j u p -> q j p u"),
+                )
+            codes = q_pool.tile([P, T], U32, name="codes", align_bytes=64)
+            scales = q_pool.tile([P, T], U8, name="scales", align_bytes=64)
+            nc.vector.quantize_mx(
+                out=codes[:].bitcast(FP8X4),
+                scales=scales[:],
+                in_=grouped[:].rearrange("q j p t -> q (j p t)"),
+            )
+
+            xsum_psum = work_psum.tile([P, CT, ONES_N], F32, tag="work")
+            for ct in range(CT):
+                for j in range(J):
+                    nc.tensor.matmul(
+                        out=xsum_psum[:, ct, :],
+                        lhsT=x_sb[:, j, ct * P : (ct + 1) * P],
+                        rhs=ones[:],
+                        start=(j == 0),
+                        stop=(j == J - 1),
+                    )
+            nc.scalar.mul(out=xm_neg[:, b, :], in_=xsum_psum[:, :, 0], mul=-1.0 / (T * B))
+            return codes, scales
+
+        def make_term(b, ct, codes, scales, term):
+            gate = gate_pool.tile([P, T], F32, name="gate")
+            for half in range(HALVES):
+                cols = slice(half * BANK, (half + 1) * BANK)
+                z = z_psum.tile([P, BANK], F32, name="z")
+                nc.tensor.matmul_mx(
+                    out=z[:],
+                    lhsT=w_words[:, ct * 2 * P : (ct + 1) * 2 * P].bitcast(FP4X4),
+                    lhsT_scale=w_scales[:, ct * P : (ct + 1) * P],
+                    rhs=codes[:, cols].bitcast(FP8X4),
+                    rhs_scale=scales[:, cols],
+                    start=True,
+                    stop=True,
+                )
+                nc.scalar.activation(
+                    out=gate[:, cols], in_=z[:], func=ACT.Sigmoid, bias=b2_col[:, ct : ct + 1], scale=1.0
+                )
+            nc.vector.scalar_tensor_tensor(
+                out=term,
+                in0=mem_neg[:, ct, :],
+                scalar=xm_neg[:, b, ct : ct + 1],
+                in1=gate[:],
+                op0=ALU.subtract,
+                op1=ALU.mult,
+            )
+
+        def open_bank(bank, pair, j0):
+            for jj in range(2):
+                nc.tensor.matmul(
+                    out=bank[:, jj, :],
+                    lhsT=ident_bf16[:],
+                    rhs=mem_sb[:, j0 + jj, pair * 2 * P : (pair + 1) * 2 * P],
+                    start=(jj == 0),
+                    stop=False,
+                )
+
+        def add_turned(bank, side, jj, block, last):
+            nc.tensor.matmul(
+                out=bank[:, jj, side * P : (side + 1) * P],
+                lhsT=block,
+                rhs=ident_f32[:],
+                is_transpose=True,
+                start=False,
+                stop=last,
+            )
+
+        def store_bank(bank, pair, j0):
+            staged = store_pool.tile([P, 2, 2 * P], F32, name="staged")
+            nc.scalar.copy(out=staged[:], in_=bank[:])
+            nc.sync.dma_start(
+                out=out_rows[:, j0 : j0 + 2, pair * 2 * P : (pair + 1) * 2 * P], in_=staged[:]
+            )
+
+        held_banks = []
+        for j0 in range(0, J, 2):
+            bank = held_psum.tile([P, 2, 2 * P], F32, name="held%d" % j0)
+            open_bank(bank, TENSOR_PAIR, j0)
+            held_banks.append(bank)
+
+        sums = [const.tile([P, T], F32, name="sum%d" % ct) for ct in range(2 * TENSOR_PAIR)]
+
+        quantised = prepare_batch(0, loaded[0], loaded[1])
+        for b in range(B):
+            codes, scales = quantised
+            if b + 1 < B:
+                loaded = load_batch(b + 1)
+                quantised = prepare_batch(b + 1, loaded[0], loaded[1])
+            waiting = None
+            for ct in range(CT):
+                if ct < 2 * TENSOR_PAIR and b == 0:
+                    make_term(b, ct, codes, scales, sums[ct][:])
+                    continue
+                term = term_pool.tile([P, T], F32, name="term")
+                make_term(b, ct, codes, scales, term[:])
+                if waiting is not None:
+                    nc.vector.tensor_add(out=sums[waiting[0]][:], in0=sums[waiting[0]][:], in1=waiting[1][:])
+                    waiting = None
+                if ct < 2 * TENSOR_PAIR:
+                    waiting = (ct, term)
+                else:
+                    side = ct - 2 * TENSOR_PAIR
+                    for j in range(J):
+                        add_turned(
+                            held_banks[j // 2],
+                            side,
+                            j % 2,
+                            term[:, j * P : (j + 1) * P],
+                            last=(b == B - 1 and side == 1 and j % 2 == 1),
+                        )
+
+        for pair in range(TENSOR_PAIR):
+            for j0 in range(0, J, 2):
+                bank = work_psum.tile([P, 2, 2 * P], F32, tag="work")
+                open_bank(bank, pair, j0)
+                for side in range(2):
+                    for jj in range(2):
+                        j = j0 + jj
+                        add_turned(
+                            bank, side, jj, sums[2 * pair + side][:, j * P : (j + 1) * P],
+                            last=(side == 1 and jj == 1),
+                        )
+                store_bank(bank, pair, j0)
+        for j0 in range(0, J, 2):
+            store_bank(held_banks[j0 // 2], TENSOR_PAIR, j0)

@@ -21,11 +21,13 @@ K = 512
 PACK = 4
 J = T // P
 CT = C // P
-PAIRS = CT // 2
+PAIR_C = 2 * P
 BANK = 512
-HALVES = T // BANK
 ONES_N = 32
-TENSOR_PAIR = PAIRS - 1
+VECTOR_TILES = 4
+FIRST_SWEEP = (0, 1, 2, 4, 5)
+SECOND_SWEEP = (3, 6, 7)
+TURN_LAG = 3
 
 FLOPS = 2 * B * T * K * C
 
@@ -40,14 +42,54 @@ def tile_dynamicmemorybank_pb_t_kernel(tc, h, x, memory, w2_words, w2_scales, b2
     with ExitStack() as ctx:
         const = ctx.enter_context(tc.tile_pool(name="const", bufs=1))
         h_pool = ctx.enter_context(tc.tile_pool(name="h_pool", bufs=2))
-        x_pool = ctx.enter_context(tc.tile_pool(name="x_pool", bufs=3))
-        q_pool = ctx.enter_context(tc.tile_pool(name="q_pool", bufs=2))
-        gate_pool = ctx.enter_context(tc.tile_pool(name="gate_pool", bufs=3))
-        term_pool = ctx.enter_context(tc.tile_pool(name="term_pool", bufs=3))
-        store_pool = ctx.enter_context(tc.tile_pool(name="store_pool", bufs=3))
-        z_psum = ctx.enter_context(tc.psum_pool(name="z_psum", bufs=2))
-        work_psum = ctx.enter_context(tc.psum_pool(name="work_psum", bufs=2))
+        x_pool = ctx.enter_context(tc.tile_pool(name="x_pool", bufs=2))
+        grouped_pool = ctx.enter_context(tc.tile_pool(name="grouped_pool", bufs=2))
+        gate_pool = ctx.enter_context(tc.tile_pool(name="gate_pool", bufs=4))
+        term_pool = ctx.enter_context(tc.tile_pool(name="term_pool", bufs=TURN_LAG + 3))
+        store_pool = ctx.enter_context(tc.tile_pool(name="store_pool", bufs=8))
+        flow_psum = ctx.enter_context(tc.psum_pool(name="flow_psum", bufs=4))
         held_psum = ctx.enter_context(tc.psum_pool(name="held_psum", bufs=1))
+        ctx.enter_context(tc.manual_schedule())
+
+        h_tiles = {}
+        x_tiles = {}
+        grouped_tiles = {}
+
+        def load_batch(b):
+            h_tiles[b] = h_pool.tile([P, J, K], BF16, name="h_sb")
+            nc.sync.dma_start(out=h_tiles[b][:], in_=h_rows[b])
+            x_tiles[b] = x_pool.tile([P, J, C], BF16, name="x_sb")
+            nc.sync.dma_start(out=x_tiles[b][:], in_=x_rows[b])
+
+        w_words = const.tile([P, 2 * C], U8, align_bytes=64)
+        w_scales = const.tile([P, C], U8, align_bytes=64)
+        b2_rows = const.tile([P, P], BF16)
+        mem_sb = const.tile([P, J, C], BF16)
+        nc.vector.memset(w_scales[:].bitcast(I32), 0)
+        nc.vector.memset(b2_rows[:], 0.0)
+
+        h_tiles[0] = h_pool.tile([P, J, K], BF16, name="h_sb")
+        nc.sync.dma_start(out=h_tiles[0][:], in_=h_rows[0])
+        nc.sync.dma_start(
+            out=w_words[:].bitcast(I32),
+            in_=w2_words.rearrange("g p n -> (g p) n").bitcast(I32),
+        )
+        scale_rows = w2_scales.rearrange("g q n -> (g q) n")
+        for quad in range(4):
+            nc.sync.dma_start(
+                out=w_scales[32 * quad : 32 * quad + 4, :].bitcast(I32),
+                in_=scale_rows[4 * quad : 4 * quad + 4, :].bitcast(I32),
+            )
+        nc.sync.dma_start(out=b2_rows[0:CT, :], in_=b2.rearrange("(r c) -> r c", r=CT))
+        x_tiles[0] = x_pool.tile([P, J, C], BF16, name="x_sb")
+        nc.sync.dma_start(out=x_tiles[0][:, :, 0 : C // 2], in_=x_rows[0, :, :, 0 : C // 2])
+        nc.sync.dma_start(out=mem_sb[:, :, 0 : C // 2], in_=mem_rows[:, :, 0 : C // 2])
+        nc.sync.dma_start(out=x_tiles[0][:, :, C // 2 : C], in_=x_rows[0, :, :, C // 2 : C])
+        h_tiles[1] = h_pool.tile([P, J, K], BF16, name="h_sb")
+        nc.sync.dma_start(out=h_tiles[1][:], in_=h_rows[1])
+        nc.sync.dma_start(out=mem_sb[:, :, C // 2 : C], in_=mem_rows[:, :, C // 2 : C])
+        x_tiles[1] = x_pool.tile([P, J, C], BF16, name="x_sb")
+        nc.sync.dma_start(out=x_tiles[1][:], in_=x_rows[1])
 
         ident_f32 = const.tile([P, P], F32)
         make_identity(nc, ident_f32[:])
@@ -55,112 +97,105 @@ def tile_dynamicmemorybank_pb_t_kernel(tc, h, x, memory, w2_words, w2_scales, b2
         make_identity(nc, ident_bf16[:])
         ones = const.tile([P, ONES_N], BF16)
         nc.vector.memset(ones[:], 1.0)
-
         warm = const.tile([P, 1], F32)
         nc.vector.memset(warm[:], 0.0)
         nc.scalar.activation(out=warm[:], in_=warm[:], func=ACT.Sigmoid)
 
-        w_words = const.tile([P, 2 * C], U8, align_bytes=64)
-        nc.sync.dma_start(
-            out=w_words[:].bitcast(I32),
-            in_=w2_words.rearrange("g p n -> (g p) n").bitcast(I32),
-        )
-        w_scales = const.tile([P, C], U8, align_bytes=64)
-        nc.vector.memset(w_scales[:].bitcast(I32), 0)
-        scale_rows = w2_scales.rearrange("g q n -> (g q) n")
-        for quad in range(4):
-            nc.sync.dma_start(
-                out=w_scales[32 * quad : 32 * quad + 4, :].bitcast(I32),
-                in_=scale_rows[4 * quad : 4 * quad + 4, :].bitcast(I32),
+        codes = const.tile([P, B, T], U32, align_bytes=64)
+        scales = const.tile([P, B, T], U8, align_bytes=64)
+        b2_col = const.tile([P, CT], F32)
+        xm_neg = const.tile([P, B, CT], F32)
+        mem_neg = const.tile([P, CT, T], BF16)
+        sums = [const.tile([P, T], F32, name="sum%d" % ct) for ct in range(VECTOR_TILES)]
+
+        def turn_h(b, piece):
+            if piece == 0:
+                grouped_tiles[b] = grouped_pool.tile([P, J, P, PACK], BF16, name="grouped", align_bytes=64)
+            h_pairs = h_tiles[b][:].bitcast(F32)
+            grouped_pairs = grouped_tiles[b][:].bitcast(F32)
+            j0 = 2 * piece
+            hT_psum = flow_psum.tile([P, 2, 2, P], F32, tag="flow")
+            for jj in range(2):
+                for u in range(2):
+                    nc.tensor.transpose(
+                        out=hT_psum[:, jj, u, :],
+                        in_=h_pairs[:, j0 + jj, u : K // 2 : 2],
+                        identity=ident_f32[:],
+                    )
+            nc.scalar.copy(
+                out=grouped_pairs[:, j0 : j0 + 2, :, :],
+                in_=hT_psum[:].rearrange("q j u p -> q j p u"),
             )
 
-        b2_rows = const.tile([P, P], BF16)
-        nc.vector.memset(b2_rows[:], 0.0)
-        nc.sync.dma_start(out=b2_rows[0:CT, :], in_=b2.rearrange("(r c) -> r c", r=CT))
-        b2_psum = work_psum.tile([P, P], BF16, tag="work")
-        nc.tensor.transpose(out=b2_psum[:], in_=b2_rows[:], identity=ident_bf16[:])
-        b2_col = const.tile([P, CT], F32)
-        nc.vector.tensor_copy(out=b2_col[:], in_=b2_psum[:, 0:CT])
+        def quantise_h(b):
+            nc.vector.quantize_mx(
+                out=codes[:, b, :].bitcast(FP8X4),
+                scales=scales[:, b, :],
+                in_=grouped_tiles[b][:].rearrange("q j p t -> q (j p t)"),
+            )
 
-        def load_batch(b):
-            h_sb = h_pool.tile([P, J, K], BF16, name="h_sb")
-            nc.sync.dma_start(out=h_sb[:], in_=h_rows[b])
-            x_sb = x_pool.tile([P, J, C], BF16, name="x_sb")
-            nc.sync.dma_start(out=x_sb[:], in_=x_rows[b])
-            return h_sb, x_sb
+        def average_x(b, half):
+            first_ct = half * (CT // 2)
+            xsum_psum = flow_psum.tile([P, CT // 2, ONES_N], F32, tag="flow")
+            for i in range(CT // 2):
+                ct = first_ct + i
+                for j in range(J):
+                    nc.tensor.matmul(
+                        out=xsum_psum[:, i, :],
+                        lhsT=x_tiles[b][:, j, ct * P : (ct + 1) * P],
+                        rhs=ones[:],
+                        start=(j == 0),
+                        stop=(j == J - 1),
+                    )
+            nc.scalar.mul(
+                out=xm_neg[:, b, first_ct : first_ct + CT // 2],
+                in_=xsum_psum[:, :, 0],
+                mul=-1.0 / (T * B),
+            )
 
-        loaded = load_batch(0)
-        mem_sb = const.tile([P, J, C], BF16)
-        nc.sync.dma_start(out=mem_sb[:], in_=mem_rows)
+        def prepare(b, part):
+            if part == 0:
+                turn_h(b, 0)
+                turn_h(b, 1)
+            elif part == 1:
+                turn_h(b, 2)
+                turn_h(b, 3)
+            elif part == 2:
+                quantise_h(b)
+                average_x(b, 0)
+            elif part == 3:
+                average_x(b, 1)
 
-        mem_neg = const.tile([P, CT, T], BF16)
-        for ct in range(CT):
-            memT_psum = work_psum.tile([P, T], BF16, tag="work")
+        def turn_memory(ct):
+            memT_psum = flow_psum.tile([P, T], BF16, tag="flow")
             for j in range(J):
                 nc.tensor.transpose(
                     out=memT_psum[:, j * P : (j + 1) * P],
                     in_=mem_sb[:, j, ct * P : (ct + 1) * P],
                     identity=ident_bf16[:],
                 )
-            nc.scalar.mul(out=mem_neg[:, ct, :], in_=memT_psum[:], mul=-1.0 / B)
+            nc.vector.tensor_scalar_mul(out=mem_neg[:, ct, :], in0=memT_psum[:], scalar1=-1.0 / B)
 
-        xm_neg = const.tile([P, B, CT], F32)
-
-        def prepare_batch(b, h_sb, x_sb):
-            h_pairs = h_sb[:].bitcast(F32)
-            grouped = q_pool.tile([P, J, P, PACK], BF16, name="grouped", align_bytes=64)
-            grouped_pairs = grouped[:].bitcast(F32)
-            for j0 in range(0, J, 2):
-                hT_psum = work_psum.tile([P, 2, 2, P], F32, tag="work")
-                for jj in range(2):
-                    for u in range(2):
-                        nc.tensor.transpose(
-                            out=hT_psum[:, jj, u, :],
-                            in_=h_pairs[:, j0 + jj, u : K // 2 : 2],
-                            identity=ident_f32[:],
-                        )
-                nc.scalar.copy(
-                    out=grouped_pairs[:, j0 : j0 + 2, :, :],
-                    in_=hT_psum[:].rearrange("q j u p -> q j p u"),
-                )
-            codes = q_pool.tile([P, T], U32, name="codes", align_bytes=64)
-            scales = q_pool.tile([P, T], U8, name="scales", align_bytes=64)
-            nc.vector.quantize_mx(
-                out=codes[:].bitcast(FP8X4),
-                scales=scales[:],
-                in_=grouped[:].rearrange("q j p t -> q (j p t)"),
-            )
-
-            xsum_psum = work_psum.tile([P, CT, ONES_N], F32, tag="work")
-            for ct in range(CT):
-                for j in range(J):
-                    nc.tensor.matmul(
-                        out=xsum_psum[:, ct, :],
-                        lhsT=x_sb[:, j, ct * P : (ct + 1) * P],
-                        rhs=ones[:],
-                        start=(j == 0),
-                        stop=(j == J - 1),
-                    )
-            nc.scalar.mul(out=xm_neg[:, b, :], in_=xsum_psum[:, :, 0], mul=-1.0 / (T * B))
-            return codes, scales
-
-        def make_term(b, ct, codes, scales, term):
+        def make_gate(b, ct):
             gate = gate_pool.tile([P, T], F32, name="gate")
-            for half in range(HALVES):
-                cols = slice(half * BANK, (half + 1) * BANK)
-                z = z_psum.tile([P, BANK], F32, name="z")
+            for first_col in range(0, T, BANK):
+                cols = slice(first_col, first_col + BANK)
+                z = flow_psum.tile([P, BANK], F32, tag="flow")
                 nc.tensor.matmul_mx(
                     out=z[:],
                     lhsT=w_words[:, ct * 2 * P : (ct + 1) * 2 * P].bitcast(FP4X4),
                     lhsT_scale=w_scales[:, ct * P : (ct + 1) * P],
-                    rhs=codes[:, cols].bitcast(FP8X4),
-                    rhs_scale=scales[:, cols],
+                    rhs=codes[:, b, cols].bitcast(FP8X4),
+                    rhs_scale=scales[:, b, cols],
                     start=True,
                     stop=True,
                 )
                 nc.scalar.activation(
                     out=gate[:, cols], in_=z[:], func=ACT.Sigmoid, bias=b2_col[:, ct : ct + 1], scale=1.0
                 )
+            return gate
+
+        def make_term(b, ct, gate, term):
             nc.vector.scalar_tensor_tensor(
                 out=term,
                 in0=mem_neg[:, ct, :],
@@ -175,7 +210,7 @@ def tile_dynamicmemorybank_pb_t_kernel(tc, h, x, memory, w2_words, w2_scales, b2
                 nc.tensor.matmul(
                     out=bank[:, jj, :],
                     lhsT=ident_bf16[:],
-                    rhs=mem_sb[:, j0 + jj, pair * 2 * P : (pair + 1) * 2 * P],
+                    rhs=mem_sb[:, j0 + jj, pair * PAIR_C : (pair + 1) * PAIR_C],
                     start=(jj == 0),
                     stop=False,
                 )
@@ -191,52 +226,36 @@ def tile_dynamicmemorybank_pb_t_kernel(tc, h, x, memory, w2_words, w2_scales, b2
             )
 
         def store_bank(bank, pair, j0):
-            staged = store_pool.tile([P, 2, 2 * P], F32, name="staged")
-            nc.scalar.copy(out=staged[:], in_=bank[:])
+            staged = store_pool.tile([P, 2, PAIR_C], F32, name="staged")
+            if (j0 // 2) % 2 == 0:
+                nc.scalar.copy(out=staged[:], in_=bank[:])
+            else:
+                nc.vector.tensor_copy(out=staged[:], in_=bank[:])
             nc.sync.dma_start(
-                out=out_rows[:, j0 : j0 + 2, pair * 2 * P : (pair + 1) * 2 * P], in_=staged[:]
+                out=out_rows[:, j0 : j0 + 2, pair * PAIR_C : (pair + 1) * PAIR_C], in_=staged[:]
             )
 
-        held_banks = []
-        for j0 in range(0, J, 2):
-            bank = held_psum.tile([P, 2, 2 * P], F32, name="held%d" % j0)
-            open_bank(bank, TENSOR_PAIR, j0)
-            held_banks.append(bank)
+        held_banks = {}
 
-        sums = [const.tile([P, T], F32, name="sum%d" % ct) for ct in range(2 * TENSOR_PAIR)]
+        def turn_term(b, ct, term):
+            pair = ct // 2
+            if b == 0 and ct % 2 == 0:
+                for j0 in range(0, J, 2):
+                    held_banks[j0] = held_psum.tile([P, 2, PAIR_C], F32, name="held%d" % j0, tag="held%d" % j0)
+                    open_bank(held_banks[j0], pair, j0)
+            closes = b == B - 1 and ct % 2 == 1
+            for j in range(J):
+                add_turned(
+                    held_banks[j - j % 2], ct % 2, j % 2, term[:, j * P : (j + 1) * P],
+                    last=(closes and j % 2 == 1),
+                )
+            if closes:
+                for j0 in range(0, J, 2):
+                    store_bank(held_banks[j0], pair, j0)
 
-        quantised = prepare_batch(0, loaded[0], loaded[1])
-        for b in range(B):
-            codes, scales = quantised
-            if b + 1 < B:
-                loaded = load_batch(b + 1)
-                quantised = prepare_batch(b + 1, loaded[0], loaded[1])
-            waiting = None
-            for ct in range(CT):
-                if ct < 2 * TENSOR_PAIR and b == 0:
-                    make_term(b, ct, codes, scales, sums[ct][:])
-                    continue
-                term = term_pool.tile([P, T], F32, name="term")
-                make_term(b, ct, codes, scales, term[:])
-                if waiting is not None:
-                    nc.vector.tensor_add(out=sums[waiting[0]][:], in0=sums[waiting[0]][:], in1=waiting[1][:])
-                    waiting = None
-                if ct < 2 * TENSOR_PAIR:
-                    waiting = (ct, term)
-                else:
-                    side = ct - 2 * TENSOR_PAIR
-                    for j in range(J):
-                        add_turned(
-                            held_banks[j // 2],
-                            side,
-                            j % 2,
-                            term[:, j * P : (j + 1) * P],
-                            last=(b == B - 1 and side == 1 and j % 2 == 1),
-                        )
-
-        for pair in range(TENSOR_PAIR):
+        def finish_vector_pair(pair):
             for j0 in range(0, J, 2):
-                bank = work_psum.tile([P, 2, 2 * P], F32, tag="work")
+                bank = flow_psum.tile([P, 2, PAIR_C], F32, tag="flow")
                 open_bank(bank, pair, j0)
                 for side in range(2):
                     for jj in range(2):
@@ -246,5 +265,51 @@ def tile_dynamicmemorybank_pb_t_kernel(tc, h, x, memory, w2_words, w2_scales, b2
                             last=(side == 1 and jj == 1),
                         )
                 store_bank(bank, pair, j0)
-        for j0 in range(0, J, 2):
-            store_bank(held_banks[j0 // 2], TENSOR_PAIR, j0)
+
+        units = [(b, ct) for b in range(B) for ct in FIRST_SWEEP]
+        units += [(b, ct) for b in range(B) for ct in SECOND_SWEEP]
+        tiles_by_first_use = FIRST_SWEEP + SECOND_SWEEP
+
+        prepare(0, 0)
+        prepare(0, 1)
+        quantise_h(0)
+        b2_psum = flow_psum.tile([P, P], BF16, tag="flow")
+        nc.tensor.transpose(out=b2_psum[:], in_=b2_rows[:], identity=ident_bf16[:])
+        nc.vector.tensor_copy(out=b2_col[:], in_=b2_psum[:, 0:CT])
+        gates = [make_gate(0, FIRST_SWEEP[0])]
+        average_x(0, 0)
+        turn_memory(tiles_by_first_use[0])
+
+        terms = []
+        for step in range(len(units) + TURN_LAG):
+            if step + 1 < len(units):
+                b, ct = units[step + 1]
+                gates.append(make_gate(b, ct))
+            if step < len(units):
+                b, ct = units[step]
+                if ct < VECTOR_TILES and b == 0:
+                    term = sums[ct]
+                else:
+                    term = term_pool.tile([P, T], F32, name="term")
+                make_term(b, ct, gates[step], term[:])
+                terms.append(term)
+            if 1 <= step <= len(units):
+                b, ct = units[step - 1]
+                if ct < VECTOR_TILES and b > 0:
+                    nc.vector.tensor_add(out=sums[ct][:], in0=sums[ct][:], in1=terms[step - 1][:])
+            if step + 1 < CT:
+                turn_memory(tiles_by_first_use[step + 1])
+            if step == 0:
+                average_x(0, 1)
+            if step < B * len(FIRST_SWEEP):
+                b, part = step // len(FIRST_SWEEP), step % len(FIRST_SWEEP)
+                if part == 0 and b + 2 < B:
+                    load_batch(b + 2)
+                if b + 1 < B:
+                    prepare(b + 1, part)
+            if step >= TURN_LAG:
+                b, ct = units[step - TURN_LAG]
+                if ct >= VECTOR_TILES:
+                    turn_term(b, ct, terms[step - TURN_LAG])
+                elif b == B - 1 and ct % 2 == 1:
+                    finish_vector_pair(ct // 2)

@@ -21,8 +21,8 @@ K = 512
 PACK = 4
 J = T // P
 CT = C // P
-PAIR_C = 2 * P
 BANK = 512
+BANK_ROWS = BANK // P
 ONES_N = 32
 VECTOR_TILES = 4
 FIRST_SWEEP = (0, 1, 2, 4, 5)
@@ -162,9 +162,8 @@ def tile_dynamicmemorybank_pb_t_kernel(tc, h, x, memory, w2_words, w2_scales, b2
                 turn_h(b, 3)
             elif part == 2:
                 quantise_h(b)
-                average_x(b, 0)
-            elif part == 3:
-                average_x(b, 1)
+            else:
+                average_x(b, part - 3)
 
         def turn_memory(ct):
             memT_psum = flow_psum.tile([P, T], BF16, tag="flow")
@@ -205,66 +204,53 @@ def tile_dynamicmemorybank_pb_t_kernel(tc, h, x, memory, w2_words, w2_scales, b2
                 op1=ALU.mult,
             )
 
-        def open_bank(bank, pair, j0):
-            for jj in range(2):
-                nc.tensor.matmul(
-                    out=bank[:, jj, :],
-                    lhsT=ident_bf16[:],
-                    rhs=mem_sb[:, j0 + jj, pair * PAIR_C : (pair + 1) * PAIR_C],
-                    start=(jj == 0),
-                    stop=False,
-                )
-
-        def add_turned(bank, side, jj, block, last):
+        def open_bank(bank, ct, j0):
             nc.tensor.matmul(
-                out=bank[:, jj, side * P : (side + 1) * P],
-                lhsT=block,
-                rhs=ident_f32[:],
-                is_transpose=True,
-                start=False,
-                stop=last,
+                out=bank[:],
+                lhsT=ident_bf16[:],
+                rhs=mem_sb[:, j0 : j0 + BANK_ROWS, ct * P : (ct + 1) * P],
+                start=True,
+                stop=False,
             )
 
-        def store_bank(bank, pair, j0):
-            staged = store_pool.tile([P, 2, PAIR_C], F32, name="staged")
-            if (j0 // 2) % 2 == 0:
+        def add_turned(bank, j0, part, last):
+            for j in range(j0, j0 + BANK_ROWS):
+                nc.tensor.matmul(
+                    out=bank[:, j - j0, :],
+                    lhsT=part[:, j * P : (j + 1) * P],
+                    rhs=ident_f32[:],
+                    is_transpose=True,
+                    start=False,
+                    stop=(last and j == j0 + BANK_ROWS - 1),
+                )
+
+        def store_bank(bank, ct, j0):
+            staged = store_pool.tile([P, BANK_ROWS, P], F32, name="staged")
+            if j0 == 0:
                 nc.scalar.copy(out=staged[:], in_=bank[:])
             else:
                 nc.vector.tensor_copy(out=staged[:], in_=bank[:])
-            nc.sync.dma_start(
-                out=out_rows[:, j0 : j0 + 2, pair * PAIR_C : (pair + 1) * PAIR_C], in_=staged[:]
-            )
+            nc.sync.dma_start(out=out_rows[:, j0 : j0 + BANK_ROWS, ct * P : (ct + 1) * P], in_=staged[:])
 
         held_banks = {}
 
         def turn_term(b, ct, term):
-            pair = ct // 2
-            if b == 0 and ct % 2 == 0:
-                for j0 in range(0, J, 2):
-                    held_banks[j0] = held_psum.tile([P, 2, PAIR_C], F32, name="held%d" % j0, tag="held%d" % j0)
-                    open_bank(held_banks[j0], pair, j0)
-            closes = b == B - 1 and ct % 2 == 1
-            for j in range(J):
-                add_turned(
-                    held_banks[j - j % 2], ct % 2, j % 2, term[:, j * P : (j + 1) * P],
-                    last=(closes and j % 2 == 1),
-                )
-            if closes:
-                for j0 in range(0, J, 2):
-                    store_bank(held_banks[j0], pair, j0)
+            for j0 in range(0, J, BANK_ROWS):
+                if b == 0:
+                    held_name = "held%d_%d" % (ct % 2, j0)
+                    held_banks[(ct, j0)] = held_psum.tile([P, BANK_ROWS, P], F32, name=held_name, tag=held_name)
+                    open_bank(held_banks[(ct, j0)], ct, j0)
+                add_turned(held_banks[(ct, j0)], j0, term, last=(b == B - 1))
+                if b == B - 1:
+                    store_bank(held_banks[(ct, j0)], ct, j0)
 
-        def finish_vector_pair(pair):
-            for j0 in range(0, J, 2):
-                bank = flow_psum.tile([P, 2, PAIR_C], F32, tag="flow")
-                open_bank(bank, pair, j0)
-                for side in range(2):
-                    for jj in range(2):
-                        j = j0 + jj
-                        add_turned(
-                            bank, side, jj, sums[2 * pair + side][:, j * P : (j + 1) * P],
-                            last=(side == 1 and jj == 1),
-                        )
-                store_bank(bank, pair, j0)
+        def finish_vector_tile(ct, last_term):
+            for j0 in range(0, J, BANK_ROWS):
+                bank = flow_psum.tile([P, BANK_ROWS, P], F32, tag="flow")
+                open_bank(bank, ct, j0)
+                add_turned(bank, j0, sums[ct], last=False)
+                add_turned(bank, j0, last_term, last=True)
+                store_bank(bank, ct, j0)
 
         units = [(b, ct) for b in range(B) for ct in FIRST_SWEEP]
         units += [(b, ct) for b in range(B) for ct in SECOND_SWEEP]
@@ -295,7 +281,7 @@ def tile_dynamicmemorybank_pb_t_kernel(tc, h, x, memory, w2_words, w2_scales, b2
                 terms.append(term)
             if 1 <= step <= len(units):
                 b, ct = units[step - 1]
-                if ct < VECTOR_TILES and b > 0:
+                if ct < VECTOR_TILES and 0 < b < B - 1:
                     nc.vector.tensor_add(out=sums[ct][:], in0=sums[ct][:], in1=terms[step - 1][:])
             if step + 1 < CT:
                 turn_memory(tiles_by_first_use[step + 1])
@@ -311,5 +297,5 @@ def tile_dynamicmemorybank_pb_t_kernel(tc, h, x, memory, w2_words, w2_scales, b2
                 b, ct = units[step - TURN_LAG]
                 if ct >= VECTOR_TILES:
                     turn_term(b, ct, terms[step - TURN_LAG])
-                elif b == B - 1 and ct % 2 == 1:
-                    finish_vector_pair(ct // 2)
+                elif b == B - 1:
+                    finish_vector_tile(ct, terms[step - TURN_LAG])

@@ -24,10 +24,15 @@ CT = C // P
 BANK = 512
 BANK_ROWS = BANK // P
 ONES_N = 32
-VECTOR_TILES = 4
-FIRST_SWEEP = (0, 1, 2, 4, 5)
-SECOND_SWEEP = (3, 6, 7)
+SWEEPS = ((0, 1, 2, 3), (4, 5), (6, 7))
+STORED = (3,)
+HELD = (7,)
+PE_LAST = {0: 0, 1: 0, 2: 0, 4: 1, 5: 1, 6: 1}
+V_PIECES = (1, 3)
 TURN_LAG = 3
+FINAL_LAG = 3
+TERM_BUFS = 8
+GATE_BUFS = 3
 
 FLOPS = 2 * B * T * K * C
 
@@ -44,20 +49,32 @@ def tile_dynamicmemorybank_pb_t_kernel(tc, h, x, memory, w2_words, w2_scales, b2
         h_pool = ctx.enter_context(tc.tile_pool(name="h_pool", bufs=2))
         x_pool = ctx.enter_context(tc.tile_pool(name="x_pool", bufs=2))
         grouped_pool = ctx.enter_context(tc.tile_pool(name="grouped_pool", bufs=2))
-        gate_pool = ctx.enter_context(tc.tile_pool(name="gate_pool", bufs=4))
-        term_pool = ctx.enter_context(tc.tile_pool(name="term_pool", bufs=TURN_LAG + 3))
-        store_pool = ctx.enter_context(tc.tile_pool(name="store_pool", bufs=8))
-        flow_psum = ctx.enter_context(tc.psum_pool(name="flow_psum", bufs=4))
-        held_psum = ctx.enter_context(tc.psum_pool(name="held_psum", bufs=1))
+        gate_pool = ctx.enter_context(tc.tile_pool(name="gate_pool", bufs=GATE_BUFS))
+        term_pool = ctx.enter_context(tc.tile_pool(name="term_pool", bufs=TERM_BUFS))
+        sum_pool = ctx.enter_context(tc.tile_pool(name="sum_pool", bufs=5))
+        store_pool = ctx.enter_context(tc.tile_pool(name="store_pool", bufs=3))
+        psum = ctx.enter_context(tc.psum_pool(name="psum", bufs=1))
         ctx.enter_context(tc.manual_schedule())
+
+        def bank_tile(i, shape, dtype):
+            return psum.tile(shape, dtype, name="bank%d" % i, tag="bank%d" % i)
+
+        flow = {"banks": [4, 5], "next": 0}
+
+        def flow_tile(shape, dtype):
+            i = flow["banks"][flow["next"] % len(flow["banks"])]
+            flow["next"] += 1
+            return bank_tile(i, shape, dtype)
 
         h_tiles = {}
         x_tiles = {}
         grouped_tiles = {}
 
-        def load_batch(b):
+        def load_h(b):
             h_tiles[b] = h_pool.tile([P, J, K], BF16, name="h_sb")
             nc.sync.dma_start(out=h_tiles[b][:], in_=h_rows[b])
+
+        def load_x(b):
             x_tiles[b] = x_pool.tile([P, J, C], BF16, name="x_sb")
             nc.sync.dma_start(out=x_tiles[b][:], in_=x_rows[b])
 
@@ -69,7 +86,8 @@ def tile_dynamicmemorybank_pb_t_kernel(tc, h, x, memory, w2_words, w2_scales, b2
         nc.vector.memset(b2_rows[:], 0.0)
 
         h_tiles[0] = h_pool.tile([P, J, K], BF16, name="h_sb")
-        nc.sync.dma_start(out=h_tiles[0][:], in_=h_rows[0])
+        nc.sync.dma_start(out=h_tiles[0][:, 0 : J // 2, :], in_=h_rows[0, :, 0 : J // 2, :])
+        nc.sync.dma_start(out=h_tiles[0][:, J // 2 : J, :], in_=h_rows[0, :, J // 2 : J, :])
         nc.sync.dma_start(
             out=w_words[:].bitcast(I32),
             in_=w2_words.rearrange("g p n -> (g p) n").bitcast(I32),
@@ -84,12 +102,11 @@ def tile_dynamicmemorybank_pb_t_kernel(tc, h, x, memory, w2_words, w2_scales, b2
         x_tiles[0] = x_pool.tile([P, J, C], BF16, name="x_sb")
         nc.sync.dma_start(out=x_tiles[0][:, :, 0 : C // 2], in_=x_rows[0, :, :, 0 : C // 2])
         nc.sync.dma_start(out=mem_sb[:, :, 0 : C // 2], in_=mem_rows[:, :, 0 : C // 2])
-        nc.sync.dma_start(out=x_tiles[0][:, :, C // 2 : C], in_=x_rows[0, :, :, C // 2 : C])
-        h_tiles[1] = h_pool.tile([P, J, K], BF16, name="h_sb")
-        nc.sync.dma_start(out=h_tiles[1][:], in_=h_rows[1])
-        nc.sync.dma_start(out=mem_sb[:, :, C // 2 : C], in_=mem_rows[:, :, C // 2 : C])
+        load_h(1)
         x_tiles[1] = x_pool.tile([P, J, C], BF16, name="x_sb")
-        nc.sync.dma_start(out=x_tiles[1][:], in_=x_rows[1])
+        nc.sync.dma_start(out=x_tiles[1][:, :, 0 : C // 2], in_=x_rows[1, :, :, 0 : C // 2])
+        nc.sync.dma_start(out=x_tiles[0][:, :, C // 2 : C], in_=x_rows[0, :, :, C // 2 : C])
+        nc.sync.dma_start(out=x_tiles[1][:, :, C // 2 : C], in_=x_rows[1, :, :, C // 2 : C])
 
         ident_f32 = const.tile([P, P], F32)
         make_identity(nc, ident_f32[:])
@@ -104,17 +121,18 @@ def tile_dynamicmemorybank_pb_t_kernel(tc, h, x, memory, w2_words, w2_scales, b2
         codes = const.tile([P, B, T], U32, align_bytes=64)
         scales = const.tile([P, B, T], U8, align_bytes=64)
         b2_col = const.tile([P, CT], F32)
-        xm_neg = const.tile([P, B, CT], F32)
-        mem_neg = const.tile([P, CT, T], BF16)
-        sums = [const.tile([P, T], F32, name="sum%d" % ct) for ct in range(VECTOR_TILES)]
+        xm = const.tile([P, B, CT], F32)
+        stored = {ct: const.tile([P, B, T], F32, name="stored%d" % ct) for ct in STORED}
+
+        hT_tiles = {}
 
         def turn_h(b, piece):
             if piece == 0:
                 grouped_tiles[b] = grouped_pool.tile([P, J, P, PACK], BF16, name="grouped", align_bytes=64)
             h_pairs = h_tiles[b][:].bitcast(F32)
-            grouped_pairs = grouped_tiles[b][:].bitcast(F32)
             j0 = 2 * piece
-            hT_psum = flow_psum.tile([P, 2, 2, P], F32, tag="flow")
+            hT_psum = bank_tile(6 + piece % 2, [P, 2, 2, P], F32)
+            hT_tiles[(b, piece)] = hT_psum
             for jj in range(2):
                 for u in range(2):
                     nc.tensor.transpose(
@@ -122,21 +140,36 @@ def tile_dynamicmemorybank_pb_t_kernel(tc, h, x, memory, w2_words, w2_scales, b2
                         in_=h_pairs[:, j0 + jj, u : K // 2 : 2],
                         identity=ident_f32[:],
                     )
-            nc.scalar.copy(
-                out=grouped_pairs[:, j0 : j0 + 2, :, :],
-                in_=hT_psum[:].rearrange("q j u p -> q j p u"),
-            )
 
-        def quantise_h(b):
+        def copy_h(b, piece):
+            grouped_pairs = grouped_tiles[b][:].bitcast(F32)
+            j0 = 2 * piece
+            hT_psum = hT_tiles[(b, piece)]
+            if piece in V_PIECES:
+                nc.vector.tensor_copy(
+                    out=grouped_pairs[:, j0 : j0 + 2, :, :],
+                    in_=hT_psum[:].rearrange("q j u p -> q j p u"),
+                )
+            else:
+                nc.scalar.copy(
+                    out=grouped_pairs[:, j0 : j0 + 2, :, :],
+                    in_=hT_psum[:].rearrange("q j u p -> q j p u"),
+                )
+
+        def quantise_h(b, half):
+            cols = slice(half * (T // 2), (half + 1) * (T // 2))
             nc.vector.quantize_mx(
-                out=codes[:, b, :].bitcast(FP8X4),
-                scales=scales[:, b, :],
-                in_=grouped_tiles[b][:].rearrange("q j p t -> q (j p t)"),
+                out=codes[:, b, cols].bitcast(FP8X4),
+                scales=scales[:, b, cols],
+                in_=grouped_tiles[b][:, half * (J // 2) : (half + 1) * (J // 2), :, :].rearrange("q j p t -> q (j p t)"),
             )
 
-        def average_x(b, half):
+        xsum_tiles = {}
+
+        def sum_x(b, half):
             first_ct = half * (CT // 2)
-            xsum_psum = flow_psum.tile([P, CT // 2, ONES_N], F32, tag="flow")
+            xsum_psum = bank_tile(7 - half, [P, CT // 2, ONES_N], F32)
+            xsum_tiles[(b, half)] = xsum_psum
             for i in range(CT // 2):
                 ct = first_ct + i
                 for j in range(J):
@@ -147,39 +180,31 @@ def tile_dynamicmemorybank_pb_t_kernel(tc, h, x, memory, w2_words, w2_scales, b2
                         start=(j == 0),
                         stop=(j == J - 1),
                     )
+
+        def mean_x(b, half):
+            first_ct = half * (CT // 2)
             nc.scalar.mul(
-                out=xm_neg[:, b, first_ct : first_ct + CT // 2],
-                in_=xsum_psum[:, :, 0],
-                mul=-1.0 / (T * B),
+                out=xm[:, b, first_ct : first_ct + CT // 2],
+                in_=xsum_tiles[(b, half)][:, :, 0],
+                mul=1.0 / T,
             )
 
-        def prepare(b, part):
-            if part == 0:
-                turn_h(b, 0)
-                turn_h(b, 1)
-            elif part == 1:
-                turn_h(b, 2)
-                turn_h(b, 3)
-            elif part == 2:
-                quantise_h(b)
-            else:
-                average_x(b, part - 3)
+        memT = {}
 
-        def turn_memory(ct):
-            memT_psum = flow_psum.tile([P, T], BF16, tag="flow")
+        def turn_memory(ct, i):
+            memT[ct] = bank_tile(i, [P, T], BF16)
             for j in range(J):
                 nc.tensor.transpose(
-                    out=memT_psum[:, j * P : (j + 1) * P],
+                    out=memT[ct][:, j * P : (j + 1) * P],
                     in_=mem_sb[:, j, ct * P : (ct + 1) * P],
                     identity=ident_bf16[:],
                 )
-            nc.vector.tensor_scalar_mul(out=mem_neg[:, ct, :], in0=memT_psum[:], scalar1=-1.0 / B)
 
         def make_gate(b, ct):
             gate = gate_pool.tile([P, T], F32, name="gate")
             for first_col in range(0, T, BANK):
                 cols = slice(first_col, first_col + BANK)
-                z = flow_psum.tile([P, BANK], F32, tag="flow")
+                z = flow_tile([P, BANK], F32)
                 nc.tensor.matmul_mx(
                     out=z[:],
                     lhsT=w_words[:, ct * 2 * P : (ct + 1) * 2 * P].bitcast(FP4X4),
@@ -197,105 +222,176 @@ def tile_dynamicmemorybank_pb_t_kernel(tc, h, x, memory, w2_words, w2_scales, b2
         def make_term(b, ct, gate, term):
             nc.vector.scalar_tensor_tensor(
                 out=term,
-                in0=mem_neg[:, ct, :],
-                scalar=xm_neg[:, b, ct : ct + 1],
+                in0=memT[ct][:],
+                scalar=xm[:, b, ct : ct + 1],
                 in1=gate[:],
                 op0=ALU.subtract,
                 op1=ALU.mult,
             )
 
-        def open_bank(bank, ct, j0):
-            nc.tensor.matmul(
-                out=bank[:],
-                lhsT=ident_bf16[:],
-                rhs=mem_sb[:, j0 : j0 + BANK_ROWS, ct * P : (ct + 1) * P],
-                start=True,
-                stop=False,
-            )
-
-        def add_turned(bank, j0, part, last):
+        def add_turned(bank, j0, part, first, last):
             for j in range(j0, j0 + BANK_ROWS):
                 nc.tensor.matmul(
                     out=bank[:, j - j0, :],
                     lhsT=part[:, j * P : (j + 1) * P],
                     rhs=ident_f32[:],
                     is_transpose=True,
-                    start=False,
+                    start=(first and j == j0),
                     stop=(last and j == j0 + BANK_ROWS - 1),
                 )
 
         def store_bank(bank, ct, j0):
             staged = store_pool.tile([P, BANK_ROWS, P], F32, name="staged")
-            if j0 == 0:
-                nc.scalar.copy(out=staged[:], in_=bank[:])
-            else:
-                nc.vector.tensor_copy(out=staged[:], in_=bank[:])
+            nc.vector.scalar_tensor_tensor(
+                out=staged[:],
+                in0=bank[:],
+                scalar=-1.0 / B,
+                in1=mem_sb[:, j0 : j0 + BANK_ROWS, ct * P : (ct + 1) * P],
+                op0=ALU.mult,
+                op1=ALU.add,
+            )
             nc.sync.dma_start(out=out_rows[:, j0 : j0 + BANK_ROWS, ct * P : (ct + 1) * P], in_=staged[:])
 
+        units = [(b, ct) for sweep in SWEEPS for b in range(B) for ct in sweep]
+        n_first = B * len(SWEEPS[0])
+        chores = []
         held_banks = {}
+        sums = {}
+        kept = {}
 
-        def turn_term(b, ct, term):
+        def final_chores(ct, parts, step):
             for j0 in range(0, J, BANK_ROWS):
-                if b == 0:
-                    held_name = "held%d_%d" % (ct % 2, j0)
-                    held_banks[(ct, j0)] = held_psum.tile([P, BANK_ROWS, P], F32, name=held_name, tag=held_name)
-                    open_bank(held_banks[(ct, j0)], ct, j0)
-                add_turned(held_banks[(ct, j0)], j0, term, last=(b == B - 1))
-                if b == B - 1:
-                    store_bank(held_banks[(ct, j0)], ct, j0)
+                def chore(j0=j0):
+                    bank = bank_tile(7, [P, BANK_ROWS, P], F32)
+                    for i, part in enumerate(parts):
+                        add_turned(bank, j0, part, i == 0, i == len(parts) - 1)
+                    store_bank(bank, ct, j0)
+                chores.append((step, chore))
 
-        def finish_vector_tile(ct, last_term):
+        def stored_chores(ct, step):
             for j0 in range(0, J, BANK_ROWS):
-                bank = flow_psum.tile([P, BANK_ROWS, P], F32, tag="flow")
-                open_bank(bank, ct, j0)
-                add_turned(bank, j0, sums[ct], last=False)
-                add_turned(bank, j0, last_term, last=True)
-                store_bank(bank, ct, j0)
+                state = {}
+                for b0 in range(0, B, 2):
+                    def chore(j0=j0, b0=b0, state=state):
+                        if b0 == 0:
+                            state["bank"] = bank_tile(7, [P, BANK_ROWS, P], F32)
+                        for b in (b0, b0 + 1):
+                            add_turned(state["bank"], j0, stored[ct][:, b, :], b == 0, b == B - 1)
+                        if b0 == B - 2:
+                            store_bank(state["bank"], ct, j0)
+                    chores.append((step, chore))
 
-        units = [(b, ct) for b in range(B) for ct in FIRST_SWEEP]
-        units += [(b, ct) for b in range(B) for ct in SECOND_SWEEP]
-        tiles_by_first_use = FIRST_SWEEP + SECOND_SWEEP
-
-        prepare(0, 0)
-        prepare(0, 1)
-        quantise_h(0)
-        b2_psum = flow_psum.tile([P, P], BF16, tag="flow")
+        turn_h(0, 0)
+        turn_h(0, 1)
+        copy_h(0, 0)
+        copy_h(0, 1)
+        turn_h(0, 2)
+        turn_h(0, 3)
+        load_h(2)
+        quantise_h(0, 0)
+        copy_h(0, 2)
+        copy_h(0, 3)
+        b2_psum = flow_tile([P, P], BF16)
         nc.tensor.transpose(out=b2_psum[:], in_=b2_rows[:], identity=ident_bf16[:])
         nc.vector.tensor_copy(out=b2_col[:], in_=b2_psum[:, 0:CT])
-        gates = [make_gate(0, FIRST_SWEEP[0])]
-        average_x(0, 0)
-        turn_memory(tiles_by_first_use[0])
+        quantise_h(0, 1)
+        gates = [make_gate(0, units[0][1])]
+        sum_x(0, 0)
+        mean_x(0, 0)
+        turn_memory(SWEEPS[0][0], 0)
 
         terms = []
-        for step in range(len(units) + TURN_LAG):
+        n1 = len(SWEEPS[0])
+
+        def first_stage(nbx):
+            return max(n1 * (nbx - 1) - 1, 0)
+
+        def second_half_step(bx):
+            return n1 * bx + (1 if bx > 0 else 2)
+
+        for step in range(len(units) + TURN_LAG + 1):
+            b1, part = step // n1, step % n1
+            nb = b1 + 1
+            sweep1 = step < n_first
+            if step == n_first - 1:
+                flow["banks"] = [4, 5, 6]
+            for nbx in range(1, B):
+                stage = step - first_stage(nbx)
+                if stage == 1:
+                    copy_h(nbx, 0)
+                    copy_h(nbx, 1)
+                elif stage == 2:
+                    copy_h(nbx, 2)
+                    copy_h(nbx, 3)
+                    quantise_h(nbx, 0)
+                elif stage == 3:
+                    quantise_h(nbx, 1)
+                if step == n1 * nbx - 1:
+                    mean_x(nbx, 0)
+            if sweep1 and step == second_half_step(b1) + 1:
+                mean_x(b1, 1)
             if step + 1 < len(units):
                 b, ct = units[step + 1]
                 gates.append(make_gate(b, ct))
             if step < len(units):
                 b, ct = units[step]
-                if ct < VECTOR_TILES and b == 0:
-                    term = sums[ct]
+                if ct in STORED:
+                    term = stored[ct][:, b, :]
+                elif ct in HELD:
+                    term = term_pool.tile([P, T], F32, name="term")[:]
+                elif b == 0:
+                    sums[ct] = sum_pool.tile([P, T], F32, name="sum")
+                    term = sums[ct][:]
                 else:
-                    term = term_pool.tile([P, T], F32, name="term")
-                make_term(b, ct, gates[step], term[:])
+                    term = term_pool.tile([P, T], F32, name="term")[:]
+                make_term(b, ct, gates[step], term)
                 terms.append(term)
             if 1 <= step <= len(units):
                 b, ct = units[step - 1]
-                if ct < VECTOR_TILES and 0 < b < B - 1:
-                    nc.vector.tensor_add(out=sums[ct][:], in0=sums[ct][:], in1=terms[step - 1][:])
-            if step + 1 < CT:
-                turn_memory(tiles_by_first_use[step + 1])
-            if step == 0:
-                average_x(0, 1)
-            if step < B * len(FIRST_SWEEP):
-                b, part = step // len(FIRST_SWEEP), step % len(FIRST_SWEEP)
-                if part == 0 and b + 2 < B:
-                    load_batch(b + 2)
-                if b + 1 < B:
-                    prepare(b + 1, part)
-            if step >= TURN_LAG:
+                if ct in PE_LAST:
+                    if 0 < b < B - PE_LAST[ct]:
+                        nc.gpsimd.tensor_tensor(out=sums[ct][:], in0=sums[ct][:], in1=terms[step - 1], op=ALU.add)
+                    elif b > 0:
+                        kept.setdefault(ct, []).append(terms[step - 1])
+                    if b == B - 1:
+                        final_chores(ct, [sums[ct][:]] + kept.get(ct, []), step + FINAL_LAG)
+                elif ct in STORED and b == B - 1:
+                    stored_chores(ct, step)
+            if step + 1 < n1:
+                turn_memory(SWEEPS[0][step + 1], step + 1)
+            for k in (1, 2):
+                first = n_first + (k - 1) * B * 2
+                for i in (0, 1):
+                    if step == first - 2 + i:
+                        turn_memory(SWEEPS[k][i], i)
+            for nbx in range(1, B):
+                stage = step - first_stage(nbx)
+                if stage == 0:
+                    turn_h(nbx, 0)
+                    turn_h(nbx, 1)
+                elif stage == 1:
+                    turn_h(nbx, 2)
+                    turn_h(nbx, 3)
+                    if nbx + 2 < B:
+                        load_h(nbx + 2)
+                if step == n1 * nbx - 2:
+                    sum_x(nbx, 0)
+            if sweep1 and step == second_half_step(b1):
+                sum_x(b1, 1)
+                if b1 + 2 < B:
+                    load_x(b1 + 2)
+                if b1 == B - 2:
+                    nc.sync.dma_start(out=mem_sb[:, :, C // 2 : C], in_=mem_rows[:, :, C // 2 : C])
+            if step >= TURN_LAG and step - TURN_LAG < len(units):
                 b, ct = units[step - TURN_LAG]
-                if ct >= VECTOR_TILES:
-                    turn_term(b, ct, terms[step - TURN_LAG])
-                elif b == B - 1:
-                    finish_vector_tile(ct, terms[step - TURN_LAG])
+                if ct in HELD:
+                    for j0 in range(0, J, BANK_ROWS):
+                        if b == 0:
+                            held_banks[(ct, j0)] = bank_tile(2 + j0 // BANK_ROWS, [P, BANK_ROWS, P], F32)
+                        add_turned(held_banks[(ct, j0)], j0, terms[step - TURN_LAG], b == 0, b == B - 1)
+                        if b == B - 1:
+                            store_bank(held_banks[(ct, j0)], ct, j0)
+            if step >= n_first and chores and chores[0][0] <= step:
+                chores.pop(0)[1]()
+        while chores:
+            chores.pop(0)[1]()

@@ -25,13 +25,19 @@ BANK = 512
 BANK_ROWS = BANK // P
 ONES_N = 32
 SWEEPS = ((0, 1, 2, 3), (4, 5), (6, 7))
-STORED = (3,)
+STORED = (0, 3)
 HELD = (7,)
-PE_LAST = {0: 0, 1: 0, 2: 0, 4: 1, 5: 1, 6: 1}
+PE_LAST = {1: 0, 2: 0, 4: 1, 5: 1, 6: 1}
 V_PIECES = (1, 3)
+LATE_Q = True
+MEM_B_STEP = 20
+STORED_RUN = 2
+AUX_BACK = 0
 TURN_LAG = 3
 FINAL_LAG = 3
-TERM_BUFS = 8
+TERM_BUFS = 5
+KEPT_BUFS = 2
+AUX_S2 = [7, 2, 3]
 GATE_BUFS = 3
 
 FLOPS = 2 * B * T * K * C
@@ -46,12 +52,13 @@ def tile_dynamicmemorybank_pb_t_kernel(tc, h, x, memory, w2_words, w2_scales, b2
 
     with ExitStack() as ctx:
         const = ctx.enter_context(tc.tile_pool(name="const", bufs=1))
-        h_pool = ctx.enter_context(tc.tile_pool(name="h_pool", bufs=2))
-        x_pool = ctx.enter_context(tc.tile_pool(name="x_pool", bufs=2))
-        grouped_pool = ctx.enter_context(tc.tile_pool(name="grouped_pool", bufs=2))
+        h_pool = ctx.enter_context(tc.tile_pool(name="h_pool", bufs=3))
+        x_pool = ctx.enter_context(tc.tile_pool(name="x_pool", bufs=3))
+        grouped_pool = ctx.enter_context(tc.tile_pool(name="grouped_pool", bufs=3))
         gate_pool = ctx.enter_context(tc.tile_pool(name="gate_pool", bufs=GATE_BUFS))
         term_pool = ctx.enter_context(tc.tile_pool(name="term_pool", bufs=TERM_BUFS))
-        sum_pool = ctx.enter_context(tc.tile_pool(name="sum_pool", bufs=5))
+        sum_pool = ctx.enter_context(tc.tile_pool(name="sum_pool", bufs=4))
+        kept_pool = ctx.enter_context(tc.tile_pool(name="kept_pool", bufs=KEPT_BUFS))
         store_pool = ctx.enter_context(tc.tile_pool(name="store_pool", bufs=3))
         psum = ctx.enter_context(tc.psum_pool(name="psum", bufs=1))
         ctx.enter_context(tc.manual_schedule())
@@ -70,13 +77,13 @@ def tile_dynamicmemorybank_pb_t_kernel(tc, h, x, memory, w2_words, w2_scales, b2
         x_tiles = {}
         grouped_tiles = {}
 
-        def load_h(b):
-            h_tiles[b] = h_pool.tile([P, J, K], BF16, name="h_sb")
-            nc.sync.dma_start(out=h_tiles[b][:], in_=h_rows[b])
+        def load_h(b, pair):
+            h_tiles[(b, pair)] = h_pool.tile([P, J // 2, K], BF16, name="h_sb")
+            nc.sync.dma_start(out=h_tiles[(b, pair)][:], in_=h_rows[b, :, pair * (J // 2) : (pair + 1) * (J // 2), :])
 
-        def load_x(b):
-            x_tiles[b] = x_pool.tile([P, J, C], BF16, name="x_sb")
-            nc.sync.dma_start(out=x_tiles[b][:], in_=x_rows[b])
+        def load_x(b, half):
+            x_tiles[(b, half)] = x_pool.tile([P, J, C // 2], BF16, name="x_sb")
+            nc.sync.dma_start(out=x_tiles[(b, half)][:], in_=x_rows[b, :, :, half * (C // 2) : (half + 1) * (C // 2)])
 
         w_words = const.tile([P, 2 * C], U8, align_bytes=64)
         w_scales = const.tile([P, C], U8, align_bytes=64)
@@ -85,9 +92,8 @@ def tile_dynamicmemorybank_pb_t_kernel(tc, h, x, memory, w2_words, w2_scales, b2
         nc.vector.memset(w_scales[:].bitcast(I32), 0)
         nc.vector.memset(b2_rows[:], 0.0)
 
-        h_tiles[0] = h_pool.tile([P, J, K], BF16, name="h_sb")
-        nc.sync.dma_start(out=h_tiles[0][:, 0 : J // 2, :], in_=h_rows[0, :, 0 : J // 2, :])
-        nc.sync.dma_start(out=h_tiles[0][:, J // 2 : J, :], in_=h_rows[0, :, J // 2 : J, :])
+        load_h(0, 0)
+        load_h(0, 1)
         nc.sync.dma_start(
             out=w_words[:].bitcast(I32),
             in_=w2_words.rearrange("g p n -> (g p) n").bitcast(I32),
@@ -99,14 +105,9 @@ def tile_dynamicmemorybank_pb_t_kernel(tc, h, x, memory, w2_words, w2_scales, b2
                 in_=scale_rows[4 * quad : 4 * quad + 4, :].bitcast(I32),
             )
         nc.sync.dma_start(out=b2_rows[0:CT, :], in_=b2.rearrange("(r c) -> r c", r=CT))
-        x_tiles[0] = x_pool.tile([P, J, C], BF16, name="x_sb")
-        nc.sync.dma_start(out=x_tiles[0][:, :, 0 : C // 2], in_=x_rows[0, :, :, 0 : C // 2])
+        load_x(0, 0)
         nc.sync.dma_start(out=mem_sb[:, :, 0 : C // 2], in_=mem_rows[:, :, 0 : C // 2])
-        load_h(1)
-        x_tiles[1] = x_pool.tile([P, J, C], BF16, name="x_sb")
-        nc.sync.dma_start(out=x_tiles[1][:, :, 0 : C // 2], in_=x_rows[1, :, :, 0 : C // 2])
-        nc.sync.dma_start(out=x_tiles[0][:, :, C // 2 : C], in_=x_rows[0, :, :, C // 2 : C])
-        nc.sync.dma_start(out=x_tiles[1][:, :, C // 2 : C], in_=x_rows[1, :, :, C // 2 : C])
+        load_h(1, 0)
 
         ident_f32 = const.tile([P, P], F32)
         make_identity(nc, ident_f32[:])
@@ -127,10 +128,10 @@ def tile_dynamicmemorybank_pb_t_kernel(tc, h, x, memory, w2_words, w2_scales, b2
         hT_tiles = {}
 
         def turn_h(b, piece):
-            if piece == 0:
-                grouped_tiles[b] = grouped_pool.tile([P, J, P, PACK], BF16, name="grouped", align_bytes=64)
-            h_pairs = h_tiles[b][:].bitcast(F32)
-            j0 = 2 * piece
+            if piece % 2 == 0:
+                grouped_tiles[(b, piece // 2)] = grouped_pool.tile([P, J // 2, P, PACK], BF16, name="grouped", align_bytes=64)
+            h_pairs = h_tiles[(b, piece // 2)][:].bitcast(F32)
+            j0 = 2 * (piece % 2)
             hT_psum = bank_tile(6 + piece % 2, [P, 2, 2, P], F32)
             hT_tiles[(b, piece)] = hT_psum
             for jj in range(2):
@@ -142,8 +143,8 @@ def tile_dynamicmemorybank_pb_t_kernel(tc, h, x, memory, w2_words, w2_scales, b2
                     )
 
         def copy_h(b, piece):
-            grouped_pairs = grouped_tiles[b][:].bitcast(F32)
-            j0 = 2 * piece
+            grouped_pairs = grouped_tiles[(b, piece // 2)][:].bitcast(F32)
+            j0 = 2 * (piece % 2)
             hT_psum = hT_tiles[(b, piece)]
             if piece in V_PIECES:
                 nc.vector.tensor_copy(
@@ -161,21 +162,21 @@ def tile_dynamicmemorybank_pb_t_kernel(tc, h, x, memory, w2_words, w2_scales, b2
             nc.vector.quantize_mx(
                 out=codes[:, b, cols].bitcast(FP8X4),
                 scales=scales[:, b, cols],
-                in_=grouped_tiles[b][:, half * (J // 2) : (half + 1) * (J // 2), :, :].rearrange("q j p t -> q (j p t)"),
+                in_=grouped_tiles[(b, half)][:].rearrange("q j p t -> q (j p t)"),
             )
 
         xsum_tiles = {}
 
         def sum_x(b, half):
             first_ct = half * (CT // 2)
-            xsum_psum = bank_tile(7 - half, [P, CT // 2, ONES_N], F32)
+            xsum_psum = bank_tile(7 if (half == 0 or b == B - 1) else 6, [P, CT // 2, ONES_N], F32)
             xsum_tiles[(b, half)] = xsum_psum
             for i in range(CT // 2):
                 ct = first_ct + i
                 for j in range(J):
                     nc.tensor.matmul(
                         out=xsum_psum[:, i, :],
-                        lhsT=x_tiles[b][:, j, ct * P : (ct + 1) * P],
+                        lhsT=x_tiles[(b, half)][:, j, i * P : (i + 1) * P],
                         rhs=ones[:],
                         start=(j == 0),
                         stop=(j == J - 1),
@@ -259,35 +260,46 @@ def tile_dynamicmemorybank_pb_t_kernel(tc, h, x, memory, w2_words, w2_scales, b2
         sums = {}
         kept = {}
 
+        aux = {"banks": [7], "next": 0}
+        finals = []
+
+        def aux_tile():
+            i = aux["banks"][aux["next"] % len(aux["banks"])]
+            aux["next"] += 1
+            return bank_tile(i, [P, BANK_ROWS, P], F32)
+
         def final_chores(ct, parts, step):
             for j0 in range(0, J, BANK_ROWS):
                 def chore(j0=j0):
-                    bank = bank_tile(7, [P, BANK_ROWS, P], F32)
+                    bank = aux_tile()
                     for i, part in enumerate(parts):
                         add_turned(bank, j0, part, i == 0, i == len(parts) - 1)
-                    store_bank(bank, ct, j0)
+                    finals.append((bank, ct, j0))
                 chores.append((step, chore))
 
         def stored_chores(ct, step):
             for j0 in range(0, J, BANK_ROWS):
                 state = {}
-                for b0 in range(0, B, 2):
+                for b0 in range(0, B, STORED_RUN):
                     def chore(j0=j0, b0=b0, state=state):
                         if b0 == 0:
-                            state["bank"] = bank_tile(7, [P, BANK_ROWS, P], F32)
-                        for b in (b0, b0 + 1):
+                            state["bank"] = aux_tile()
+                        for b in range(b0, b0 + STORED_RUN):
                             add_turned(state["bank"], j0, stored[ct][:, b, :], b == 0, b == B - 1)
-                        if b0 == B - 2:
-                            store_bank(state["bank"], ct, j0)
+                        if b0 == B - STORED_RUN:
+                            finals.append((state["bank"], ct, j0))
                     chores.append((step, chore))
 
         turn_h(0, 0)
         turn_h(0, 1)
+        load_h(1, 1)
+        load_x(1, 0)
+        load_x(0, 1)
         copy_h(0, 0)
         copy_h(0, 1)
         turn_h(0, 2)
         turn_h(0, 3)
-        load_h(2)
+        load_h(2, 0)
         quantise_h(0, 0)
         copy_h(0, 2)
         copy_h(0, 3)
@@ -297,6 +309,7 @@ def tile_dynamicmemorybank_pb_t_kernel(tc, h, x, memory, w2_words, w2_scales, b2
         quantise_h(0, 1)
         gates = [make_gate(0, units[0][1])]
         sum_x(0, 0)
+        load_x(2, 0)
         mean_x(0, 0)
         turn_memory(SWEEPS[0][0], 0)
 
@@ -307,7 +320,7 @@ def tile_dynamicmemorybank_pb_t_kernel(tc, h, x, memory, w2_words, w2_scales, b2
             return max(n1 * (nbx - 1) - 1, 0)
 
         def second_half_step(bx):
-            return n1 * bx + (1 if bx > 0 else 2)
+            return min(n1 * (bx + 1) + 1, n_first - 1)
 
         for step in range(len(units) + TURN_LAG + 1):
             b1, part = step // n1, step % n1
@@ -315,6 +328,13 @@ def tile_dynamicmemorybank_pb_t_kernel(tc, h, x, memory, w2_words, w2_scales, b2
             sweep1 = step < n_first
             if step == n_first - 1:
                 flow["banks"] = [4, 5, 6]
+            if step == n_first:
+                aux["banks"] = AUX_S2
+                aux["next"] = 0
+            if step == n_first + 2 * B - AUX_BACK:
+                aux["banks"] = [7]
+            while finals:
+                store_bank(*finals.pop(0))
             for nbx in range(1, B):
                 stage = step - first_stage(nbx)
                 if stage == 1:
@@ -323,13 +343,17 @@ def tile_dynamicmemorybank_pb_t_kernel(tc, h, x, memory, w2_words, w2_scales, b2
                 elif stage == 2:
                     copy_h(nbx, 2)
                     copy_h(nbx, 3)
-                    quantise_h(nbx, 0)
+                    if not LATE_Q:
+                        quantise_h(nbx, 0)
                 elif stage == 3:
+                    if LATE_Q:
+                        quantise_h(nbx, 0)
                     quantise_h(nbx, 1)
                 if step == n1 * nbx - 1:
                     mean_x(nbx, 0)
-            if sweep1 and step == second_half_step(b1) + 1:
-                mean_x(b1, 1)
+            for bx in range(B):
+                if step == second_half_step(bx) + 1:
+                    mean_x(bx, 1)
             if step + 1 < len(units):
                 b, ct = units[step + 1]
                 gates.append(make_gate(b, ct))
@@ -342,6 +366,8 @@ def tile_dynamicmemorybank_pb_t_kernel(tc, h, x, memory, w2_words, w2_scales, b2
                 elif b == 0:
                     sums[ct] = sum_pool.tile([P, T], F32, name="sum")
                     term = sums[ct][:]
+                elif b >= B - PE_LAST[ct]:
+                    term = kept_pool.tile([P, T], F32, name="kept")[:]
                 else:
                     term = term_pool.tile([P, T], F32, name="term")[:]
                 make_term(b, ct, gates[step], term)
@@ -369,19 +395,23 @@ def tile_dynamicmemorybank_pb_t_kernel(tc, h, x, memory, w2_words, w2_scales, b2
                 if stage == 0:
                     turn_h(nbx, 0)
                     turn_h(nbx, 1)
+                    if nbx + 1 < B:
+                        load_h(nbx + 1, 1)
                 elif stage == 1:
                     turn_h(nbx, 2)
                     turn_h(nbx, 3)
                     if nbx + 2 < B:
-                        load_h(nbx + 2)
+                        load_h(nbx + 2, 0)
                 if step == n1 * nbx - 2:
                     sum_x(nbx, 0)
-            if sweep1 and step == second_half_step(b1):
-                sum_x(b1, 1)
-                if b1 + 2 < B:
-                    load_x(b1 + 2)
-                if b1 == B - 2:
-                    nc.sync.dma_start(out=mem_sb[:, :, C // 2 : C], in_=mem_rows[:, :, C // 2 : C])
+                    load_x(nbx, 1)
+            for bx in range(B):
+                if step == second_half_step(bx):
+                    sum_x(bx, 1)
+                    if bx + 3 < B:
+                        load_x(bx + 3, 0)
+            if step == MEM_B_STEP:
+                nc.sync.dma_start(out=mem_sb[:, :, C // 2 : C], in_=mem_rows[:, :, C // 2 : C])
             if step >= TURN_LAG and step - TURN_LAG < len(units):
                 b, ct = units[step - TURN_LAG]
                 if ct in HELD:
@@ -390,8 +420,11 @@ def tile_dynamicmemorybank_pb_t_kernel(tc, h, x, memory, w2_words, w2_scales, b2
                             held_banks[(ct, j0)] = bank_tile(2 + j0 // BANK_ROWS, [P, BANK_ROWS, P], F32)
                         add_turned(held_banks[(ct, j0)], j0, terms[step - TURN_LAG], b == 0, b == B - 1)
                         if b == B - 1:
-                            store_bank(held_banks[(ct, j0)], ct, j0)
+                            finals.append((held_banks[(ct, j0)], ct, j0))
             if step >= n_first and chores and chores[0][0] <= step:
                 chores.pop(0)[1]()
-        while chores:
-            chores.pop(0)[1]()
+        while chores or finals:
+            while finals:
+                store_bank(*finals.pop(0))
+            if chores:
+                chores.pop(0)[1]()

@@ -25,18 +25,20 @@ BANK = 512
 BANK_ROWS = BANK // P
 ONES_N = 32
 SWEEPS = ((0, 1, 2, 3), (4, 5), (6, 7))
-STORED = (0, 3)
+STORED = (2, 3)
 HELD = (7,)
-PE_LAST = {1: 0, 2: 0, 4: 1, 5: 1, 6: 1}
+PE_LAST = {0: 0, 1: 0, 4: 1, 5: 1, 6: 1}
 V_PIECES = (1, 3)
 LATE_Q = True
+MEM_BANKS = {1: (0, 1), 2: (2, 3)}
+MEM_AHEAD = {1: 2, 2: 3}
+HELD_BANKS = (0, 1)
 MEM_B_STEP = 20
 STORED_RUN = 2
-AUX_BACK = 0
+AUX_BACK = 5
 TURN_LAG = 3
 FINAL_LAG = 3
 TERM_BUFS = 5
-KEPT_BUFS = 2
 AUX_S2 = [7, 2, 3]
 GATE_BUFS = 3
 
@@ -58,8 +60,7 @@ def tile_dynamicmemorybank_pb_t_kernel(tc, h, x, memory, w2_words, w2_scales, b2
         gate_pool = ctx.enter_context(tc.tile_pool(name="gate_pool", bufs=GATE_BUFS))
         term_pool = ctx.enter_context(tc.tile_pool(name="term_pool", bufs=TERM_BUFS))
         sum_pool = ctx.enter_context(tc.tile_pool(name="sum_pool", bufs=4))
-        kept_pool = ctx.enter_context(tc.tile_pool(name="kept_pool", bufs=KEPT_BUFS))
-        store_pool = ctx.enter_context(tc.tile_pool(name="store_pool", bufs=3))
+        store_pool = ctx.enter_context(tc.tile_pool(name="store_pool", bufs=4))
         psum = ctx.enter_context(tc.psum_pool(name="psum", bufs=1))
         ctx.enter_context(tc.manual_schedule())
 
@@ -259,6 +260,7 @@ def tile_dynamicmemorybank_pb_t_kernel(tc, h, x, memory, w2_words, w2_scales, b2
         held_banks = {}
         sums = {}
         kept = {}
+        kept_slots = {"next": 0}
 
         aux = {"banks": [7], "next": 0}
         finals = []
@@ -333,6 +335,9 @@ def tile_dynamicmemorybank_pb_t_kernel(tc, h, x, memory, w2_words, w2_scales, b2
                 aux["next"] = 0
             if step == n_first + 2 * B - AUX_BACK:
                 aux["banks"] = [7]
+            if step == len(units):
+                aux["banks"] = [7, 4, 5, 6]
+                aux["next"] = 0
             while finals:
                 store_bank(*finals.pop(0))
             for nbx in range(1, B):
@@ -351,12 +356,12 @@ def tile_dynamicmemorybank_pb_t_kernel(tc, h, x, memory, w2_words, w2_scales, b2
                     quantise_h(nbx, 1)
                 if step == n1 * nbx - 1:
                     mean_x(nbx, 0)
-            for bx in range(B):
-                if step == second_half_step(bx) + 1:
-                    mean_x(bx, 1)
             if step + 1 < len(units):
                 b, ct = units[step + 1]
                 gates.append(make_gate(b, ct))
+            for bx in range(B):
+                if step == second_half_step(bx) + 1:
+                    mean_x(bx, 1)
             if step < len(units):
                 b, ct = units[step]
                 if ct in STORED:
@@ -367,7 +372,8 @@ def tile_dynamicmemorybank_pb_t_kernel(tc, h, x, memory, w2_words, w2_scales, b2
                     sums[ct] = sum_pool.tile([P, T], F32, name="sum")
                     term = sums[ct][:]
                 elif b >= B - PE_LAST[ct]:
-                    term = kept_pool.tile([P, T], F32, name="kept")[:]
+                    term = stored[STORED[0]][:, kept_slots["next"] % B, :]
+                    kept_slots["next"] += 1
                 else:
                     term = term_pool.tile([P, T], F32, name="term")[:]
                 make_term(b, ct, gates[step], term)
@@ -388,8 +394,8 @@ def tile_dynamicmemorybank_pb_t_kernel(tc, h, x, memory, w2_words, w2_scales, b2
             for k in (1, 2):
                 first = n_first + (k - 1) * B * 2
                 for i in (0, 1):
-                    if step == first - 2 + i:
-                        turn_memory(SWEEPS[k][i], i)
+                    if step == first - MEM_AHEAD[k] + i:
+                        turn_memory(SWEEPS[k][i], MEM_BANKS[k][i])
             for nbx in range(1, B):
                 stage = step - first_stage(nbx)
                 if stage == 0:
@@ -417,7 +423,7 @@ def tile_dynamicmemorybank_pb_t_kernel(tc, h, x, memory, w2_words, w2_scales, b2
                 if ct in HELD:
                     for j0 in range(0, J, BANK_ROWS):
                         if b == 0:
-                            held_banks[(ct, j0)] = bank_tile(2 + j0 // BANK_ROWS, [P, BANK_ROWS, P], F32)
+                            held_banks[(ct, j0)] = bank_tile(HELD_BANKS[j0 // BANK_ROWS], [P, BANK_ROWS, P], F32)
                         add_turned(held_banks[(ct, j0)], j0, terms[step - TURN_LAG], b == 0, b == B - 1)
                         if b == B - 1:
                             finals.append((held_banks[(ct, j0)], ct, j0))

@@ -30,6 +30,7 @@ HELD = (7,)
 PE_LAST = {0: 0, 1: 0, 4: 1, 5: 1, 6: 1}
 V_PIECES = (1, 3)
 LATE_Q = True
+PAIRED = {2: 2}
 MEM_BANKS = {1: (0, 1), 2: (2, 3)}
 MEM_AHEAD = {1: 2, 2: 3}
 HELD_BANKS = (0, 1)
@@ -37,8 +38,8 @@ MEM_B_STEP = 20
 STORED_RUN = 2
 AUX_BACK = 5
 TURN_LAG = 3
-FINAL_LAG = 3
-TERM_BUFS = 5
+FINAL_LAG = 7
+TERM_BUFS = 7
 AUX_S2 = [7, 2, 3]
 GATE_BUFS = 3
 
@@ -280,15 +281,16 @@ def tile_dynamicmemorybank_pb_t_kernel(tc, h, x, memory, w2_words, w2_scales, b2
                 chores.append((step, chore))
 
         def stored_chores(ct, step):
+            slots = list(range(0, B, PAIRED.get(ct, 1)))
             for j0 in range(0, J, BANK_ROWS):
                 state = {}
-                for b0 in range(0, B, STORED_RUN):
-                    def chore(j0=j0, b0=b0, state=state):
-                        if b0 == 0:
+                for i0 in range(0, len(slots), STORED_RUN):
+                    def chore(j0=j0, i0=i0, state=state):
+                        if i0 == 0:
                             state["bank"] = aux_tile()
-                        for b in range(b0, b0 + STORED_RUN):
-                            add_turned(state["bank"], j0, stored[ct][:, b, :], b == 0, b == B - 1)
-                        if b0 == B - STORED_RUN:
+                        for i in range(i0, i0 + STORED_RUN):
+                            add_turned(state["bank"], j0, stored[ct][:, slots[i], :], i == 0, i == len(slots) - 1)
+                        if i0 == len(slots) - STORED_RUN:
                             finals.append((state["bank"], ct, j0))
                     chores.append((step, chore))
 
@@ -387,8 +389,14 @@ def tile_dynamicmemorybank_pb_t_kernel(tc, h, x, memory, w2_words, w2_scales, b2
                         kept.setdefault(ct, []).append(terms[step - 1])
                     if b == B - 1:
                         final_chores(ct, [sums[ct][:]] + kept.get(ct, []), step + FINAL_LAG)
-                elif ct in STORED and b == B - 1:
-                    stored_chores(ct, step)
+                elif ct in STORED:
+                    group = PAIRED.get(ct, 1)
+                    if b % group > 0:
+                        nc.gpsimd.tensor_tensor(
+                            out=stored[ct][:, b - b % group, :], in0=stored[ct][:, b - b % group, :], in1=stored[ct][:, b, :], op=ALU.add
+                        )
+                    if b == B - 1:
+                        stored_chores(ct, step + (FINAL_LAG if group > 1 else 0))
             if step + 1 < n1:
                 turn_memory(SWEEPS[0][step + 1], step + 1)
             for k in (1, 2):

@@ -28,7 +28,7 @@ SWEEPS = ((0, 1, 2, 3), (4, 5), (6, 7))
 STORED = (2, 3)
 HELD = (7,)
 PE_LAST = {0: 0, 1: 0, 4: 1, 5: 1, 6: 1}
-V_PIECES = (1, 3)
+V_PIECES = (0, 2)
 LATE_Q = True
 PAIRED = {2: 2}
 MEM_BANKS = {1: (0, 1), 2: (2, 3)}
@@ -38,10 +38,11 @@ MEM_B_STEP = 20
 STORED_RUN = 2
 AUX_BACK = 5
 TURN_LAG = 3
-FINAL_LAG = 7
+FINAL_LAG = 6
 TERM_BUFS = 7
 AUX_S2 = [7, 2, 3]
 GATE_BUFS = 3
+LATE_X = {6: 34, 7: 37}
 
 FLOPS = 2 * B * T * K * C
 
@@ -171,7 +172,10 @@ def tile_dynamicmemorybank_pb_t_kernel(tc, h, x, memory, w2_words, w2_scales, b2
 
         def sum_x(b, half):
             first_ct = half * (CT // 2)
-            xsum_psum = bank_tile(7 if (half == 0 or b == B - 1) else 6, [P, CT // 2, ONES_N], F32)
+            if half == 1 and b in LATE_X:
+                xsum_psum = aux_tile((P, CT // 2, ONES_N))
+            else:
+                xsum_psum = bank_tile(7 if half == 0 else 6, [P, CT // 2, ONES_N], F32)
             xsum_tiles[(b, half)] = xsum_psum
             for i in range(CT // 2):
                 ct = first_ct + i
@@ -266,10 +270,10 @@ def tile_dynamicmemorybank_pb_t_kernel(tc, h, x, memory, w2_words, w2_scales, b2
         aux = {"banks": [7], "next": 0}
         finals = []
 
-        def aux_tile():
+        def aux_tile(shape=(P, BANK_ROWS, P)):
             i = aux["banks"][aux["next"] % len(aux["banks"])]
             aux["next"] += 1
-            return bank_tile(i, [P, BANK_ROWS, P], F32)
+            return bank_tile(i, list(shape), F32)
 
         def final_chores(ct, parts, step):
             for j0 in range(0, J, BANK_ROWS):
@@ -324,7 +328,7 @@ def tile_dynamicmemorybank_pb_t_kernel(tc, h, x, memory, w2_words, w2_scales, b2
             return max(n1 * (nbx - 1) - 1, 0)
 
         def second_half_step(bx):
-            return min(n1 * (bx + 1) + 1, n_first - 1)
+            return LATE_X.get(bx, n1 * (bx + 1) + 1)
 
         for step in range(len(units) + TURN_LAG + 1):
             b1, part = step // n1, step % n1

from contextlib import ExitStack

import concourse.mybir as mybir
from concourse.masks import make_identity

F32 = mybir.dt.float32
BF16 = mybir.dt.bfloat16
I32 = mybir.dt.int32
U32 = mybir.dt.uint32
U8 = mybir.dt.uint8
FP8X4 = mybir.dt.float8_e4m3fn_x4
FP4X4 = mybir.dt.float4_e2m1fn_x4
ALU = mybir.AluOpType
ACT = mybir.ActivationFunctionType

P = 128
B = 8
T = 1024
C = 1024
K = 512
PACK = 4
J = T // P
CT = C // P
BANK = 512
BANK_ROWS = BANK // P
ONES_N = 32
SWEEPS = ((0, 1, 2, 3), (4, 5), (6, 7))
STORED = (2, 3)
HELD = (7,)
PE_LAST = {0: 0, 1: 0, 4: 1, 5: 1, 6: 1}
V_PIECES = (0, 2)
LATE_Q = True
PAIRED = {2: 2}
MEM_BANKS = {1: (0, 1), 2: (2, 3)}
MEM_AHEAD = {1: 2, 2: 3}
HELD_BANKS = (0, 1)
MEM_B_STEP = 20
STORED_RUN = 2
AUX_BACK = 5
TURN_LAG = 3
FINAL_LAG = 6
TERM_BUFS = 7
AUX_S2 = [7, 2, 3]
GATE_BUFS = 3
LATE_X = {6: 34, 7: 37}

FLOPS = 2 * B * T * K * C


def tile_dynamicmemorybank_pb_t_kernel(tc, h, x, memory, w2_words, w2_scales, b2, out):
    nc = tc.nc
    h_rows = h.rearrange("b (p j) k -> b p j k", j=J)
    x_rows = x.rearrange("b (p j) c -> b p j c", j=J)
    mem_rows = memory.rearrange("o (p j) c -> (o p) j c", j=J)
    out_rows = out.rearrange("o (p j) c -> (o p) j c", j=J)

    with ExitStack() as ctx:
        const = ctx.enter_context(tc.tile_pool(name="const", bufs=1))
        h_pool = ctx.enter_context(tc.tile_pool(name="h_pool", bufs=3))
        x_pool = ctx.enter_context(tc.tile_pool(name="x_pool", bufs=3))
        grouped_pool = ctx.enter_context(tc.tile_pool(name="grouped_pool", bufs=3))
        gate_pool = ctx.enter_context(tc.tile_pool(name="gate_pool", bufs=GATE_BUFS))
        term_pool = ctx.enter_context(tc.tile_pool(name="term_pool", bufs=TERM_BUFS))
        sum_pool = ctx.enter_context(tc.tile_pool(name="sum_pool", bufs=4))
        store_pool = ctx.enter_context(tc.tile_pool(name="store_pool", bufs=4))
        psum = ctx.enter_context(tc.psum_pool(name="psum", bufs=1))
        ctx.enter_context(tc.manual_schedule())

        def bank_tile(i, shape, dtype):
            return psum.tile(shape, dtype, name="bank%d" % i, tag="bank%d" % i)

        flow = {"banks": [4, 5], "next": 0}

        def flow_tile(shape, dtype):
            i = flow["banks"][flow["next"] % len(flow["banks"])]
            flow["next"] += 1
            return bank_tile(i, shape, dtype)

        h_tiles = {}
        x_tiles = {}
        grouped_tiles = {}

        def load_h(b, pair):
            h_tiles[(b, pair)] = h_pool.tile([P, J // 2, K], BF16, name="h_sb")
            nc.sync.dma_start(out=h_tiles[(b, pair)][:], in_=h_rows[b, :, pair * (J // 2) : (pair + 1) * (J // 2), :])

        def load_x(b, half):
            x_tiles[(b, half)] = x_pool.tile([P, J, C // 2], BF16, name="x_sb")
            nc.sync.dma_start(out=x_tiles[(b, half)][:], in_=x_rows[b, :, :, half * (C // 2) : (half + 1) * (C // 2)])

        w_words = const.tile([P, 2 * C], U8, align_bytes=64)
        w_scales = const.tile([P, C], U8, align_bytes=64)
        b2_rows = const.tile([P, P], BF16)
        mem_sb = const.tile([P, J, C], BF16)
        nc.vector.memset(w_scales[:].bitcast(I32), 0)
        nc.vector.memset(b2_rows[:], 0.0)

        load_h(0, 0)
        load_h(0, 1)
        nc.sync.dma_start(
            out=w_words[:].bitcast(I32),
            in_=w2_words.rearrange("g p n -> (g p) n").bitcast(I32),
        )
        scale_rows = w2_scales.rearrange("g q n -> (g q) n")
        for quad in range(4):
            nc.sync.dma_start(
                out=w_scales[32 * quad : 32 * quad + 4, :].bitcast(I32),
                in_=scale_rows[4 * quad : 4 * quad + 4, :].bitcast(I32),
            )
        nc.sync.dma_start(out=b2_rows[0:CT, :], in_=b2.rearrange("(r c) -> r c", r=CT))
        load_x(0, 0)
        nc.sync.dma_start(out=mem_sb[:, :, 0 : C // 2], in_=mem_rows[:, :, 0 : C // 2])
        load_h(1, 0)

        ident_f32 = const.tile([P, P], F32)
        make_identity(nc, ident_f32[:])
        ident_bf16 = const.tile([P, P], BF16)
        make_identity(nc, ident_bf16[:])
        ones = const.tile([P, ONES_N], BF16)
        nc.vector.memset(ones[:], 1.0)
        warm = const.tile([P, 1], F32)
        nc.vector.memset(warm[:], 0.0)
        nc.scalar.activation(out=warm[:], in_=warm[:], func=ACT.Sigmoid)

        codes = const.tile([P, B, T], U32, align_bytes=64)
        scales = const.tile([P, B, T], U8, align_bytes=64)
        b2_col = const.tile([P, CT], F32)
        xm = const.tile([P, B, CT], F32)
        stored = {ct: const.tile([P, B, T], F32, name="stored%d" % ct) for ct in STORED}

        hT_tiles = {}

        def turn_h(b, piece):
            if piece % 2 == 0:
                grouped_tiles[(b, piece // 2)] = grouped_pool.tile([P, J // 2, P, PACK], BF16, name="grouped", align_bytes=64)
            h_pairs = h_tiles[(b, piece // 2)][:].bitcast(F32)
            j0 = 2 * (piece % 2)
            hT_psum = bank_tile(6 + piece % 2, [P, 2, 2, P], F32)
            hT_tiles[(b, piece)] = hT_psum
            for jj in range(2):
                for u in range(2):
                    nc.tensor.transpose(
                        out=hT_psum[:, jj, u, :],
                        in_=h_pairs[:, j0 + jj, u : K // 2 : 2],
                        identity=ident_f32[:],
                    )

        def copy_h(b, piece):
            grouped_pairs = grouped_tiles[(b, piece // 2)][:].bitcast(F32)
            j0 = 2 * (piece % 2)
            hT_psum = hT_tiles[(b, piece)]
            if piece in V_PIECES:
                nc.vector.tensor_copy(
                    out=grouped_pairs[:, j0 : j0 + 2, :, :],
                    in_=hT_psum[:].rearrange("q j u p -> q j p u"),
                )
            else:
                nc.scalar.copy(
                    out=grouped_pairs[:, j0 : j0 + 2, :, :],
                    in_=hT_psum[:].rearrange("q j u p -> q j p u"),
                )

        def quantise_h(b, half):
            cols = slice(half * (T // 2), (half + 1) * (T // 2))
            nc.vector.quantize_mx(
                out=codes[:, b, cols].bitcast(FP8X4),
                scales=scales[:, b, cols],
                in_=grouped_tiles[(b, half)][:].rearrange("q j p t -> q (j p t)"),
            )

        xsum_tiles = {}

        def sum_x(b, half):
            first_ct = half * (CT // 2)
            if half == 1 and b in LATE_X:
                xsum_psum = aux_tile((P, CT // 2, ONES_N))
            else:
                xsum_psum = bank_tile(7 if half == 0 else 6, [P, CT // 2, ONES_N], F32)
            xsum_tiles[(b, half)] = xsum_psum
            for i in range(CT // 2):
                ct = first_ct + i
                for j in range(J):
                    nc.tensor.matmul(
                        out=xsum_psum[:, i, :],
                        lhsT=x_tiles[(b, half)][:, j, i * P : (i + 1) * P],
                        rhs=ones[:],
                        start=(j == 0),
                        stop=(j == J - 1),
                    )

        def mean_x(b, half):
            first_ct = half * (CT // 2)
            nc.scalar.mul(
                out=xm[:, b, first_ct : first_ct + CT // 2],
                in_=xsum_tiles[(b, half)][:, :, 0],
                mul=1.0 / T,
            )

        memT = {}

        def turn_memory(ct, i):
            memT[ct] = bank_tile(i, [P, T], BF16)
            for j in range(J):
                nc.tensor.transpose(
                    out=memT[ct][:, j * P : (j + 1) * P],
                    in_=mem_sb[:, j, ct * P : (ct + 1) * P],
                    identity=ident_bf16[:],
                )

        def make_gate(b, ct):
            gate = gate_pool.tile([P, T], F32, name="gate")
            for first_col in range(0, T, BANK):
                cols = slice(first_col, first_col + BANK)
                z = flow_tile([P, BANK], F32)
                nc.tensor.matmul_mx(
                    out=z[:],
                    lhsT=w_words[:, ct * 2 * P : (ct + 1) * 2 * P].bitcast(FP4X4),
                    lhsT_scale=w_scales[:, ct * P : (ct + 1) * P],
                    rhs=codes[:, b, cols].bitcast(FP8X4),
                    rhs_scale=scales[:, b, cols],
                    start=True,
                    stop=True,
                )
                nc.scalar.activation(
                    out=gate[:, cols], in_=z[:], func=ACT.Sigmoid, bias=b2_col[:, ct : ct + 1], scale=1.0
                )
            return gate

        def make_term(b, ct, gate, term):
            nc.vector.scalar_tensor_tensor(
                out=term,
                in0=memT[ct][:],
                scalar=xm[:, b, ct : ct + 1],
                in1=gate[:],
                op0=ALU.subtract,
                op1=ALU.mult,
            )

        def add_turned(bank, j0, part, first, last):
            for j in range(j0, j0 + BANK_ROWS):
                nc.tensor.matmul(
                    out=bank[:, j - j0, :],
                    lhsT=part[:, j * P : (j + 1) * P],
                    rhs=ident_f32[:],
                    is_transpose=True,
                    start=(first and j == j0),
                    stop=(last and j == j0 + BANK_ROWS - 1),
                )

        def store_bank(bank, ct, j0):
            staged = store_pool.tile([P, BANK_ROWS, P], F32, name="staged")
            nc.vector.scalar_tensor_tensor(
                out=staged[:],
                in0=bank[:],
                scalar=-1.0 / B,
                in1=mem_sb[:, j0 : j0 + BANK_ROWS, ct * P : (ct + 1) * P],
                op0=ALU.mult,
                op1=ALU.add,
            )
            nc.sync.dma_start(out=out_rows[:, j0 : j0 + BANK_ROWS, ct * P : (ct + 1) * P], in_=staged[:])

        units = [(b, ct) for sweep in SWEEPS for b in range(B) for ct in sweep]
        n_first = B * len(SWEEPS[0])
        chores = []
        held_banks = {}
        sums = {}
        kept = {}
        kept_slots = {"next": 0}

        aux = {"banks": [7], "next": 0}
        finals = []

        def aux_tile(shape=(P, BANK_ROWS, P)):
            i = aux["banks"][aux["next"] % len(aux["banks"])]
            aux["next"] += 1
            return bank_tile(i, list(shape), F32)

        def final_chores(ct, parts, step):
            for j0 in range(0, J, BANK_ROWS):
                def chore(j0=j0):
                    bank = aux_tile()
                    for i, part in enumerate(parts):
                        add_turned(bank, j0, part, i == 0, i == len(parts) - 1)
                    finals.append((bank, ct, j0))
                chores.append((step, chore))

        def stored_chores(ct, step):
            slots = list(range(0, B, PAIRED.get(ct, 1)))
            for j0 in range(0, J, BANK_ROWS):
                state = {}
                for i0 in range(0, len(slots), STORED_RUN):
                    def chore(j0=j0, i0=i0, state=state):
                        if i0 == 0:
                            state["bank"] = aux_tile()
                        for i in range(i0, i0 + STORED_RUN):
                            add_turned(state["bank"], j0, stored[ct][:, slots[i], :], i == 0, i == len(slots) - 1)
                        if i0 == len(slots) - STORED_RUN:
                            finals.append((state["bank"], ct, j0))
                    chores.append((step, chore))

        turn_h(0, 0)
        turn_h(0, 1)
        load_h(1, 1)
        load_x(1, 0)
        load_x(0, 1)
        copy_h(0, 0)
        copy_h(0, 1)
        turn_h(0, 2)
        turn_h(0, 3)
        load_h(2, 0)
        quantise_h(0, 0)
        copy_h(0, 2)
        copy_h(0, 3)
        b2_psum = flow_tile([P, P], BF16)
        nc.tensor.transpose(out=b2_psum[:], in_=b2_rows[:], identity=ident_bf16[:])
        nc.vector.tensor_copy(out=b2_col[:], in_=b2_psum[:, 0:CT])
        quantise_h(0, 1)
        gates = [make_gate(0, units[0][1])]
        sum_x(0, 0)
        load_x(2, 0)
        mean_x(0, 0)
        turn_memory(SWEEPS[0][0], 0)

        terms = []
        n1 = len(SWEEPS[0])

        def first_stage(nbx):
            return max(n1 * (nbx - 1) - 1, 0)

        def second_half_step(bx):
            return LATE_X.get(bx, n1 * (bx + 1) + 1)

        for step in range(len(units) + TURN_LAG + 1):
            b1, part = step // n1, step % n1
            nb = b1 + 1
            sweep1 = step < n_first
            if step == n_first - 1:
                flow["banks"] = [4, 5, 6]
            if step == n_first:
                aux["banks"] = AUX_S2
                aux["next"] = 0
            if step == n_first + 2 * B - AUX_BACK:
                aux["banks"] = [7]
            if step == len(units):
                aux["banks"] = [7, 4, 5, 6]
                aux["next"] = 0
            while finals:
                store_bank(*finals.pop(0))
            for nbx in range(1, B):
                stage = step - first_stage(nbx)
                if stage == 1:
                    copy_h(nbx, 0)
                    copy_h(nbx, 1)
                elif stage == 2:
                    copy_h(nbx, 2)
                    copy_h(nbx, 3)
                    if not LATE_Q:
                        quantise_h(nbx, 0)
                elif stage == 3:
                    if LATE_Q:
                        quantise_h(nbx, 0)
                    quantise_h(nbx, 1)
                if step == n1 * nbx - 1:
                    mean_x(nbx, 0)
            if step + 1 < len(units):
                b, ct = units[step + 1]
                gates.append(make_gate(b, ct))
            for bx in range(B):
                if step == second_half_step(bx) + 1:
                    mean_x(bx, 1)
            if step < len(units):
                b, ct = units[step]
                if ct in STORED:
                    term = stored[ct][:, b, :]
                elif ct in HELD:
                    term = term_pool.tile([P, T], F32, name="term")[:]
                elif b == 0:
                    sums[ct] = sum_pool.tile([P, T], F32, name="sum")
                    term = sums[ct][:]
                elif b >= B - PE_LAST[ct]:
                    term = stored[STORED[0]][:, kept_slots["next"] % B, :]
                    kept_slots["next"] += 1
                else:
                    term = term_pool.tile([P, T], F32, name="term")[:]
                make_term(b, ct, gates[step], term)
                terms.append(term)
            if 1 <= step <= len(units):
                b, ct = units[step - 1]
                if ct in PE_LAST:
                    if 0 < b < B - PE_LAST[ct]:
                        nc.gpsimd.tensor_tensor(out=sums[ct][:], in0=sums[ct][:], in1=terms[step - 1], op=ALU.add)
                    elif b > 0:
                        kept.setdefault(ct, []).append(terms[step - 1])
                    if b == B - 1:
                        final_chores(ct, [sums[ct][:]] + kept.get(ct, []), step + FINAL_LAG)
                elif ct in STORED:
                    group = PAIRED.get(ct, 1)
                    if b % group > 0:
                        nc.gpsimd.tensor_tensor(
                            out=stored[ct][:, b - b % group, :], in0=stored[ct][:, b - b % group, :], in1=stored[ct][:, b, :], op=ALU.add
                        )
                    if b == B - 1:
                        stored_chores(ct, step + (FINAL_LAG if group > 1 else 0))
            if step + 1 < n1:
                turn_memory(SWEEPS[0][step + 1], step + 1)
            for k in (1, 2):
                first = n_first + (k - 1) * B * 2
                for i in (0, 1):
                    if step == first - MEM_AHEAD[k] + i:
                        turn_memory(SWEEPS[k][i], MEM_BANKS[k][i])
            for nbx in range(1, B):
                stage = step - first_stage(nbx)
                if stage == 0:
                    turn_h(nbx, 0)
                    turn_h(nbx, 1)
                    if nbx + 1 < B:
                        load_h(nbx + 1, 1)
                elif stage == 1:
                    turn_h(nbx, 2)
                    turn_h(nbx, 3)
                    if nbx + 2 < B:
                        load_h(nbx + 2, 0)
                if step == n1 * nbx - 2:
                    sum_x(nbx, 0)
                    load_x(nbx, 1)
            for bx in range(B):
                if step == second_half_step(bx):
                    sum_x(bx, 1)
                    if bx + 3 < B:
                        load_x(bx + 3, 0)
            if step == MEM_B_STEP:
                nc.sync.dma_start(out=mem_sb[:, :, C // 2 : C], in_=mem_rows[:, :, C // 2 : C])
            if step >= TURN_LAG and step - TURN_LAG < len(units):
                b, ct = units[step - TURN_LAG]
                if ct in HELD:
                    for j0 in range(0, J, BANK_ROWS):
                        if b == 0:
                            held_banks[(ct, j0)] = bank_tile(HELD_BANKS[j0 // BANK_ROWS], [P, BANK_ROWS, P], F32)
                        add_turned(held_banks[(ct, j0)], j0, terms[step - TURN_LAG], b == 0, b == B - 1)
                        if b == B - 1:
                            finals.append((held_banks[(ct, j0)], ct, j0))
            if step >= n_first and chores and chores[0][0] <= step:
                chores.pop(0)[1]()
        while chores or finals:
            while finals:
                store_bank(*finals.pop(0))
            if chores:
                chores.pop(0)[1]()
